import numpy as np
import ml_dtypes


def mxq(x, axis, fmt="e4m3"):
    dtype, down = {"e4m3": (ml_dtypes.float8_e4m3fn, 7), "e5m2": (ml_dtypes.float8_e5m2, 14)}[fmt]
    v = np.moveaxis(np.asarray(x, np.float32).astype(ml_dtypes.bfloat16).astype(np.float64), axis, -1)
    blocks = v.reshape(v.shape[:-1] + (-1, 32))
    amax = np.abs(blocks).max(-1, keepdims=True)
    byte = np.maximum(np.where(amax > 0, np.frexp(amax)[1] - 1 + 127, 0) - down, 1)
    scale = np.exp2(byte - 127.0)
    codes = (blocks / scale).astype(np.float32).astype(dtype).astype(np.float64)
    return np.moveaxis((codes * scale).reshape(v.shape), -1, axis)


WIDE = False


def mx_kscale(k):
    if not WIDE:
        return np.ones(k)
    levels = np.array([10, -10, 5, -5, 0])
    a = np.random.permutation(np.resize(levels, k // 512 * 4)).reshape(k // 512, 4)
    idx = np.arange(k)
    return np.exp2(a[idx // 512, idx % 128 // 32])


BF16 = ml_dtypes.bfloat16


def bf(x):
    return np.asarray(x, np.float32).astype(BF16)


def f64(x):
    return np.asarray(x).astype(np.float64)


B, I, H, O = 128, 512, 1024, 512
RHO_OVER_T = 1.68e-8 / 35e-6
MIN_TRACE_W, MAX_TRACE_W = 0.09, 5.0
W_MIN, W_MAX = -3.0, 3.0
BOARD = 2800.0 * np.sqrt(H)


def manhattan(a, b):
    return np.sum(np.abs(a[:, None, :] - b[None, :, :]), axis=-1)


def effective_weight(W, L):
    norm = (np.clip(W, W_MIN, W_MAX) - W_MIN) / (W_MAX - W_MIN)
    width = MIN_TRACE_W + norm * (MAX_TRACE_W - MIN_TRACE_W)
    R = RHO_OVER_T * L / width
    return W * (1.0 / (R + 1.0))


def sigmoid(v):
    return 1.0 / (1.0 + np.exp(-v))


def setup_inputs():
    s = mx_kscale(I)
    x = bf(np.random.standard_normal((B, I)) * 0.23 * np.sqrt(H / I) * s)
    W1 = bf(np.random.standard_normal((I, H)) * 1.5 / s[:, None])
    b1 = bf(np.random.standard_normal(H) * 0.5)
    W2 = bf(np.random.standard_normal((H, O)) * 1.5 - 1.0)
    input_positions = bf(np.random.random((I, 2)) * np.array([0.4 * BOARD, BOARD]))
    hidden_positions = bf(np.random.random((H, 2)) * np.array([0.6 * BOARD, BOARD]) + np.array([0.2 * BOARD, 0.0]))
    output_positions = bf(np.random.random((O, 2)) * np.array([0.4 * BOARD, BOARD]) + np.array([0.6 * BOARD, 0.0]))
    drive = 0.5 * effective_weight(f64(W2), manhattan(f64(hidden_positions), f64(output_positions))).sum(0)
    b2 = bf(np.random.standard_normal(O) * 0.5 - drive)
    return {"x": x, "W1": W1, "b1": b1, "W2": W2, "b2": b2, "input_positions": input_positions,
            "hidden_positions": hidden_positions, "output_positions": output_positions}


def reference(x, W1, b1, W2, b2, input_positions, hidden_positions, output_positions):
    L1 = manhattan(f64(input_positions), f64(hidden_positions))
    L2 = manhattan(f64(hidden_positions), f64(output_positions))
    W1_eff = effective_weight(f64(W1), L1)
    W2_eff = effective_weight(f64(W2), L2)
    hidden = sigmoid((mxq(f64(x), 1, "e4m3") @ mxq(W1_eff, 0, "e4m3")) + f64(b1))
    return sigmoid((mxq(hidden, 1, "e4m3") @ mxq(W2_eff, 0, "e4m3")) + f64(b2))

@@ -1,0 +1,247 @@
+from contextlib import ExitStack
+
+import concourse.mybir as mybir
+from concourse.masks import make_identity
+
+F32 = mybir.dt.float32
+BF16 = mybir.dt.bfloat16
+U32 = mybir.dt.uint32
+U8 = mybir.dt.uint8
+FP8X4 = mybir.dt.float8_e4m3fn_x4
+ALU = mybir.AluOpType
+FUNC = mybir.ActivationFunctionType
+
+P = 128
+PACK = 4
+K_PASS = P * PACK
+B, I, H, O = 128, 512, 1024, 512
+H_PASSES = H // K_PASS
+COLS = 256
+
+RHO_OVER_T = 1.68e-8 / 35e-6
+W_LIMIT = 3.0
+WIDTH_SLOPE = (5.0 - 0.09) / (2.0 * W_LIMIT)
+WIDTH_MID = 0.09 + W_LIMIT * WIDTH_SLOPE
+BETA = WIDTH_MID / WIDTH_SLOPE
+LENGTH_SCALE = RHO_OVER_T / WIDTH_SLOPE
+
+FLOPS = 2 * B * I * H + 2 * B * H * O
+
+
+def effective_weight_chunk(nc, work, w_rows, row_pos, neg_col_pos, eff_out):
+    dist_x = work.tile([P, PACK, COLS], F32)
+    dist_y = work.tile([P, PACK, COLS], F32)
+    for j in range(PACK):
+        nc.scalar.activation(
+            out=dist_x[:, j, :], in_=row_pos[:, :, 0], func=FUNC.Abs, bias=neg_col_pos[:, j, 0:1]
+        )
+        nc.scalar.activation(
+            out=dist_y[:, j, :], in_=row_pos[:, :, 1], func=FUNC.Abs, bias=neg_col_pos[:, j, 1:2]
+        )
+
+    clipped = work.tile([P, PACK, COLS], BF16)
+    nc.vector.tensor_scalar(
+        out=clipped[:], in0=w_rows, scalar1=-W_LIMIT, scalar2=W_LIMIT, op0=ALU.max, op1=ALU.min
+    )
+    numer = work.tile([P, PACK, COLS], F32)
+    nc.vector.scalar_tensor_tensor(
+        out=numer[:], in0=clipped[:], scalar=BETA, in1=w_rows, op0=ALU.add, op1=ALU.mult
+    )
+    length = work.tile([P, PACK, COLS], F32)
+    nc.vector.scalar_tensor_tensor(
+        out=length[:],
+        in0=dist_x[:],
+        scalar=BETA / LENGTH_SCALE,
+        in1=dist_y[:],
+        op0=ALU.add,
+        op1=ALU.add,
+    )
+    denom = work.tile([P, PACK, COLS], F32)
+    nc.vector.scalar_tensor_tensor(
+        out=denom[:],
+        in0=clipped[:],
+        scalar=1.0 / LENGTH_SCALE,
+        in1=length[:],
+        op0=ALU.mult,
+        op1=ALU.add,
+    )
+
+    rsqrt = work.tile([P, PACK, COLS], F32)
+    nc.scalar.activation(
+        out=rsqrt[:], in_=denom[:], func=FUNC.Abs_reciprocal_sqrt, scale=LENGTH_SCALE
+    )
+    recip = work.tile([P, PACK, COLS], F32)
+    nc.scalar.activation(out=recip[:], in_=rsqrt[:], func=FUNC.Square)
+
+    nc.vector.tensor_tensor(
+        out=eff_out,
+        in0=numer[:].rearrange("p j (a i) -> p a j i", i=4),
+        in1=recip[:].rearrange("p j (a i) -> p a j i", i=4),
+        op=ALU.mult,
+    )
+
+
+def tile_physicalneuralnetwork_s_kernel(
+    tc, x, W1, b1, W2, b2, input_positions, hidden_positions, output_positions, out
+):
+    nc = tc.nc
+    with ExitStack() as stack:
+        keep = stack.enter_context(tc.tile_pool(name="keep", bufs=1))
+        work = stack.enter_context(tc.tile_pool(name="work", bufs=3))
+        psum = stack.enter_context(tc.psum_pool(name="psum", bufs=1))
+
+        in_col = keep.tile([P, PACK, 2], BF16)
+        nc.sync.dma_start(
+            out=in_col[:], in_=input_positions.rearrange("(p j) c -> p j c", j=PACK)
+        )
+        hid_row = keep.tile([P, H * 2], BF16)
+        w1_sb = keep.tile([P, PACK, H], BF16)
+        for g in range(H_PASSES):
+            h_cols = slice(g * K_PASS, (g + 1) * K_PASS)
+            nc.sync.dma_start(
+                out=hid_row[:, 2 * g * K_PASS : 2 * (g + 1) * K_PASS],
+                in_=hidden_positions[h_cols, :].rearrange("h c -> (h c)").partition_broadcast(P),
+            )
+            nc.sync.dma_start(
+                out=w1_sb[:, :, h_cols],
+                in_=W1.rearrange("(p j) h -> p j h", j=PACK)[:, :, h_cols],
+            )
+        x_sb = keep.tile([P, I], BF16)
+        nc.sync.dma_start(out=x_sb[:], in_=x)
+        hid_col = keep.tile([P, H_PASSES, PACK, 2], BF16)
+        nc.sync.dma_start(
+            out=hid_col[:],
+            in_=hidden_positions.rearrange("(g p j) c -> p g j c", g=H_PASSES, j=PACK),
+        )
+        out_row = keep.tile([P, O * 2], BF16)
+        nc.sync.dma_start(
+            out=out_row[:], in_=output_positions.rearrange("o c -> (o c)").partition_broadcast(P)
+        )
+        w2_sb = keep.tile([P, H_PASSES, PACK, O], BF16)
+        for g in range(H_PASSES):
+            nc.sync.dma_start(
+                out=w2_sb[:, g, :, :],
+                in_=W2[g * K_PASS : (g + 1) * K_PASS, :].rearrange("(p j) o -> p j o", j=PACK),
+            )
+        b1_bf = keep.tile([P, H_PASSES, PACK], BF16)
+        nc.sync.dma_start(out=b1_bf[:], in_=b1.rearrange("(g p t) -> p g t", g=H_PASSES, t=PACK))
+        b2_row = keep.tile([P, O], BF16)
+        nc.sync.dma_start(out=b2_row[:], in_=b2.partition_broadcast(P))
+
+        identity = keep.tile([P, P], F32)
+        make_identity(nc, identity[:])
+
+        neg_in_col = keep.tile([P, PACK, 2], F32)
+        nc.vector.tensor_scalar_mul(out=neg_in_col[:], in0=in_col[:], scalar1=-1.0)
+        neg_hid_col = keep.tile([P, H_PASSES, PACK, 2], F32)
+        nc.vector.tensor_scalar_mul(out=neg_hid_col[:], in0=hid_col[:], scalar1=-1.0)
+        b1_col = keep.tile([P, H_PASSES, PACK], F32)
+        nc.vector.tensor_copy(out=b1_col[:], in_=b1_bf[:])
+
+        x_words = x_sb[:].bitcast(F32).rearrange("b (p u) -> b u p", u=2)
+        xT_ps = psum.tile([P, 2, B], F32)
+        for u in range(2):
+            nc.tensor.transpose(out=xT_ps[:, u, :], in_=x_words[:, u, :], identity=identity[:])
+        x_grouped = keep.tile([P, B * PACK], BF16, align_bytes=64)
+        nc.vector.tensor_copy(
+            out=x_grouped[:].bitcast(F32).rearrange("p (b u) -> p b u", u=2),
+            in_=xT_ps[:].rearrange("p u b -> p b u"),
+        )
+        x_codes = keep.tile([P, B], U32, align_bytes=64)
+        x_scales = keep.tile([P, B], U8, align_bytes=64)
+        nc.vector.quantize_mx(out=x_codes[:].bitcast(FP8X4), scales=x_scales[:], in_=x_grouped[:])
+
+        w1_grouped = keep.tile([P, H_PASSES, PACK, P, PACK], BF16, align_bytes=64)
+        w1_codes = keep.tile([P, H], U32, align_bytes=64)
+        w1_scales = keep.tile([P, H], U8, align_bytes=64)
+        hid_row_xy = hid_row[:].rearrange("p (h c) -> p h c", c=2)
+        for g in range(H_PASSES):
+            for part in range(K_PASS // COLS):
+                h_cols = slice(g * K_PASS + part * COLS, g * K_PASS + (part + 1) * COLS)
+                q_range = slice(part * COLS // PACK, (part + 1) * COLS // PACK)
+                effective_weight_chunk(
+                    nc,
+                    work,
+                    w_rows=w1_sb[:, :, h_cols],
+                    row_pos=hid_row_xy[:, h_cols, :],
+                    neg_col_pos=neg_in_col[:],
+                    eff_out=w1_grouped[:, g, :, q_range, :].rearrange("p t q j -> p q j t"),
+                )
+            g_cols = slice(g * K_PASS, (g + 1) * K_PASS)
+            nc.vector.quantize_mx(
+                out=w1_codes[:, g_cols].bitcast(FP8X4),
+                scales=w1_scales[:, g_cols],
+                in_=w1_grouped[:, g].rearrange("p t q j -> p (t q j)"),
+            )
+
+        hid_pre = keep.tile([P, H_PASSES, B, PACK], F32)
+        for g in range(H_PASSES):
+            hid_ps = psum.tile([P, PACK, B], F32, name="hid_ps%d" % g)
+            for t in range(PACK):
+                unit_cols = slice((g * PACK + t) * P, (g * PACK + t + 1) * P)
+                nc.tensor.matmul_mx(
+                    out=hid_ps[:, t, :],
+                    lhsT=w1_codes[:, unit_cols].bitcast(FP8X4),
+                    lhsT_scale=w1_scales[:, unit_cols],
+                    rhs=x_codes[:].bitcast(FP8X4),
+                    rhs_scale=x_scales[:],
+                    start=True,
+                    stop=True,
+                )
+            nc.vector.tensor_tensor(
+                out=hid_pre[:, g],
+                in0=hid_ps[:].rearrange("q t b -> q b t"),
+                in1=b1_col[:, g, :].unsqueeze(1).to_broadcast([P, B, PACK]),
+                op=ALU.add,
+            )
+
+        w2_grouped = keep.tile([P, H_PASSES, O, PACK], BF16, align_bytes=64)
+        w2_codes = keep.tile([P, H_PASSES, O], U32, align_bytes=64)
+        w2_scales = keep.tile([P, H_PASSES, O], U8, align_bytes=64)
+        out_row_xy = out_row[:].rearrange("p (o c) -> p o c", c=2)
+        for g in range(H_PASSES):
+            for part in range(O // COLS):
+                o_cols = slice(part * COLS, (part + 1) * COLS)
+                effective_weight_chunk(
+                    nc,
+                    work,
+                    w_rows=w2_sb[:, g, :, o_cols],
+                    row_pos=out_row_xy[:, o_cols, :],
+                    neg_col_pos=neg_hid_col[:, g],
+                    eff_out=w2_grouped[:, g, o_cols, :].rearrange("p (a i) j -> p a j i", i=4),
+                )
+                nc.vector.quantize_mx(
+                    out=w2_codes[:, g, o_cols].bitcast(FP8X4),
+                    scales=w2_scales[:, g, o_cols],
+                    in_=w2_grouped[:, g, o_cols, :].rearrange("p o j -> p (o j)"),
+                )
+
+        hid_bf = keep.tile([P, H_PASSES, B * PACK], BF16, align_bytes=64)
+        hid_codes = keep.tile([P, H_PASSES, B], U32, align_bytes=64)
+        hid_scales = keep.tile([P, H_PASSES, B], U8, align_bytes=64)
+        for g in range(H_PASSES):
+            nc.scalar.activation(
+                out=hid_bf[:, g, :],
+                in_=hid_pre[:, g].rearrange("q b t -> q (b t)"),
+                func=FUNC.Sigmoid,
+            )
+            nc.vector.quantize_mx(
+                out=hid_codes[:, g, :].bitcast(FP8X4), scales=hid_scales[:, g, :], in_=hid_bf[:, g, :]
+            )
+
+        out_ps = psum.tile([P, O], F32)
+        for g in range(H_PASSES):
+            nc.tensor.matmul_mx(
+                out=out_ps[:],
+                lhsT=hid_codes[:, g, :].bitcast(FP8X4),
+                lhsT_scale=hid_scales[:, g, :],
+                rhs=w2_codes[:, g, :].bitcast(FP8X4),
+                rhs_scale=w2_scales[:, g, :],
+                start=(g == 0),
+                stop=(g == H_PASSES - 1),
+            )
+        out_pre = keep.tile([P, O], F32)
+        nc.vector.tensor_tensor(out=out_pre[:], in0=out_ps[:], in1=b2_row[:], op=ALU.add)
+        out_sb = keep.tile([P, O], F32)
+        nc.scalar.activation(out=out_sb[:], in_=out_pre[:], func=FUNC.Sigmoid)
+        nc.sync.dma_start(out=out, in_=out_sb[:])

@@ -1,3 +1,4 @@
+import math
 from contextlib import ExitStack
 
 import concourse.mybir as mybir
@@ -17,6 +18,8 @@ K_PASS = P * PACK
 B, I, H, O = 128, 512, 1024, 512
 H_PASSES = H // K_PASS
 COLS = 256
+COL_BLOCKS = COLS // P
+VECTOR_SQUARES_EVERY = 4
 
 RHO_OVER_T = 1.68e-8 / 35e-6
 W_LIMIT = 3.0
@@ -28,55 +31,81 @@ LENGTH_SCALE = RHO_OVER_T / WIDTH_SLOPE
 FLOPS = 2 * B * I * H + 2 * B * H * O
 
 
-def effective_weight_chunk(nc, work, w_rows, row_pos, neg_col_pos, eff_out):
-    dist_x = work.tile([P, PACK, COLS], F32)
-    dist_y = work.tile([P, PACK, COLS], F32)
-    for j in range(PACK):
-        nc.scalar.activation(
-            out=dist_x[:, j, :], in_=row_pos[:, :, 0], func=FUNC.Abs, bias=neg_col_pos[:, j, 0:1]
-        )
-        nc.scalar.activation(
-            out=dist_y[:, j, :], in_=row_pos[:, :, 1], func=FUNC.Abs, bias=neg_col_pos[:, j, 1:2]
-        )
-
-    clipped = work.tile([P, PACK, COLS], BF16)
+def effective_weight_chunk(
+    nc, pools, consts, w_rows, k_pos, neg_col_pos, eff_out, square_on_vector
+):
+    clipped = pools["work"].tile([P, PACK, COLS], BF16)
     nc.vector.tensor_scalar(
         out=clipped[:], in0=w_rows, scalar1=-W_LIMIT, scalar2=W_LIMIT, op0=ALU.max, op1=ALU.min
     )
-    numer = work.tile([P, PACK, COLS], F32)
+    numer = pools["work"].tile([P, PACK, COLS], F32)
     nc.vector.scalar_tensor_tensor(
         out=numer[:], in0=clipped[:], scalar=BETA, in1=w_rows, op0=ALU.add, op1=ALU.mult
     )
-    length = work.tile([P, PACK, COLS], F32)
-    nc.vector.scalar_tensor_tensor(
-        out=length[:],
-        in0=dist_x[:],
-        scalar=BETA / LENGTH_SCALE,
-        in1=dist_y[:],
-        op0=ALU.add,
-        op1=ALU.add,
-    )
-    denom = work.tile([P, PACK, COLS], F32)
-    nc.vector.scalar_tensor_tensor(
-        out=denom[:],
-        in0=clipped[:],
-        scalar=1.0 / LENGTH_SCALE,
-        in1=length[:],
-        op0=ALU.mult,
-        op1=ALU.add,
-    )
 
-    rsqrt = work.tile([P, PACK, COLS], F32)
+    denom = pools["work"].tile([P, PACK, COLS], F32)
+    for u in range(COL_BLOCKS):
+        dist_x = pools["dist"].tile([P, K_PASS], F32)
+        dist_y = pools["dist"].tile([P, K_PASS], F32)
+        nc.scalar.activation(
+            out=dist_x[:], in_=k_pos[:, :, 0], func=FUNC.Abs, bias=neg_col_pos[:, u, 0:1]
+        )
+        nc.scalar.activation(
+            out=dist_y[:], in_=k_pos[:, :, 1], func=FUNC.Abs, bias=neg_col_pos[:, u, 1:2]
+        )
+        length_ps = pools["length"].tile([P, PACK, P], F32)
+        for j in range(PACK):
+            k_cols = slice(j * P, (j + 1) * P)
+            nc.tensor.matmul(
+                out=length_ps[:, j, :],
+                lhsT=dist_x[:, k_cols],
+                rhs=consts["identity"],
+                is_transpose=True,
+                start=True,
+                stop=False,
+            )
+            nc.tensor.matmul(
+                out=length_ps[:, j, :],
+                lhsT=dist_y[:, k_cols],
+                rhs=consts["identity"],
+                is_transpose=True,
+                start=False,
+                stop=True,
+            )
+        u_cols = slice(u * P, (u + 1) * P)
+        nc.vector.scalar_tensor_tensor(
+            out=denom[:, :, u_cols],
+            in0=length_ps[:],
+            scalar=LENGTH_SCALE,
+            in1=clipped[:, :, u_cols],
+            op0=ALU.mult,
+            op1=ALU.add,
+        )
+
+    rsqrt = pools["work"].tile([P, PACK, COLS], F32)
     nc.scalar.activation(
-        out=rsqrt[:], in_=denom[:], func=FUNC.Abs_reciprocal_sqrt, scale=LENGTH_SCALE
+        out=rsqrt[:],
+        in_=denom[:],
+        func=FUNC.Abs_reciprocal_sqrt,
+        scale=1.0 / BETA,
+        bias=consts["one"],
     )
-    recip = work.tile([P, PACK, COLS], F32)
-    nc.scalar.activation(out=recip[:], in_=rsqrt[:], func=FUNC.Square)
+    first = pools["work"].tile([P, PACK, COLS], F32)
+    if square_on_vector:
+        nc.vector.scalar_tensor_tensor(
+            out=first[:], in0=numer[:], scalar=1.0 / BETA, in1=rsqrt[:], op0=ALU.mult, op1=ALU.mult
+        )
+        second = rsqrt
+    else:
+        nc.scalar.activation(
+            out=first[:], in_=rsqrt[:], func=FUNC.Square, scale=1.0 / math.sqrt(BETA)
+        )
+        second = numer
 
     nc.vector.tensor_tensor(
-        out=eff_out,
-        in0=numer[:].rearrange("p j (a i) -> p a j i", i=4),
-        in1=recip[:].rearrange("p j (a i) -> p a j i", i=4),
+        out=eff_out.rearrange("p (a i) j -> p a j i", i=4),
+        in0=first[:].rearrange("p j (a i) -> p a j i", i=4),
+        in1=second[:].rearrange("p j (a i) -> p a j i", i=4),
         op=ALU.mult,
     )
 
@@ -87,91 +116,98 @@ def tile_physicalneuralnetwork_s_kernel(
     nc = tc.nc
     with ExitStack() as stack:
         keep = stack.enter_context(tc.tile_pool(name="keep", bufs=1))
-        work = stack.enter_context(tc.tile_pool(name="work", bufs=3))
+        pools = {
+            "work": stack.enter_context(tc.tile_pool(name="work", bufs=3)),
+            "dist": stack.enter_context(tc.tile_pool(name="dist", bufs=6)),
+            "length": stack.enter_context(tc.psum_pool(name="length", bufs=4)),
+        }
         psum = stack.enter_context(tc.psum_pool(name="psum", bufs=1))
 
-        in_col = keep.tile([P, PACK, 2], BF16)
+        hid_blk = keep.tile([P, H // P, 2], BF16)
+        nc.scalar.dma_start(out=hid_blk[:], in_=hidden_positions.rearrange("(m r) c -> r m c", r=P))
+        out_blk = keep.tile([P, O // P, 2], BF16)
+        nc.scalar.dma_start(out=out_blk[:], in_=output_positions.rearrange("(m r) c -> r m c", r=P))
+        b1_bf = keep.tile([P, H // P], BF16)
+        with nc.allow_non_contiguous_dma(reason="1,024 bias values, one to a partition and block"):
+            nc.scalar.dma_start(out=b1_bf[:], in_=b1.rearrange("(m r) -> r m", r=P))
+
+        one = keep.tile([P, 1], F32)
+        nc.vector.memset(one[:], 1.0)
+        table_warmer = keep.tile([P, 1], F32)
+        nc.scalar.activation(out=table_warmer[:], in_=one[:], func=FUNC.Abs_reciprocal_sqrt)
+
+        in_row = keep.tile([P, I * 2], BF16)
         nc.sync.dma_start(
-            out=in_col[:], in_=input_positions.rearrange("(p j) c -> p j c", j=PACK)
+            out=in_row[:], in_=input_positions.rearrange("i c -> (i c)").partition_broadcast(P)
         )
-        hid_row = keep.tile([P, H * 2], BF16)
         w1_sb = keep.tile([P, PACK, H], BF16)
-        for g in range(H_PASSES):
-            h_cols = slice(g * K_PASS, (g + 1) * K_PASS)
+        for half in range(2):
+            h_cols = slice(half * H // 2, (half + 1) * H // 2)
             nc.sync.dma_start(
-                out=hid_row[:, 2 * g * K_PASS : 2 * (g + 1) * K_PASS],
-                in_=hidden_positions[h_cols, :].rearrange("h c -> (h c)").partition_broadcast(P),
-            )
-            nc.sync.dma_start(
-                out=w1_sb[:, :, h_cols],
-                in_=W1.rearrange("(p j) h -> p j h", j=PACK)[:, :, h_cols],
+                out=w1_sb[:, :, h_cols], in_=W1.rearrange("(j p) h -> p j h", p=P)[:, :, h_cols]
             )
         x_sb = keep.tile([P, I], BF16)
         nc.sync.dma_start(out=x_sb[:], in_=x)
-        hid_col = keep.tile([P, H_PASSES, PACK, 2], BF16)
+        hid_row = keep.tile([P, H * 2], BF16)
         nc.sync.dma_start(
-            out=hid_col[:],
-            in_=hidden_positions.rearrange("(g p j) c -> p g j c", g=H_PASSES, j=PACK),
-        )
-        out_row = keep.tile([P, O * 2], BF16)
-        nc.sync.dma_start(
-            out=out_row[:], in_=output_positions.rearrange("o c -> (o c)").partition_broadcast(P)
+            out=hid_row[:], in_=hidden_positions.rearrange("h c -> (h c)").partition_broadcast(P)
         )
         w2_sb = keep.tile([P, H_PASSES, PACK, O], BF16)
         for g in range(H_PASSES):
             nc.sync.dma_start(
                 out=w2_sb[:, g, :, :],
-                in_=W2[g * K_PASS : (g + 1) * K_PASS, :].rearrange("(p j) o -> p j o", j=PACK),
+                in_=W2[g * K_PASS : (g + 1) * K_PASS, :].rearrange("(j p) o -> p j o", p=P),
             )
-        b1_bf = keep.tile([P, H_PASSES, PACK], BF16)
-        nc.sync.dma_start(out=b1_bf[:], in_=b1.rearrange("(g p t) -> p g t", g=H_PASSES, t=PACK))
         b2_row = keep.tile([P, O], BF16)
         nc.sync.dma_start(out=b2_row[:], in_=b2.partition_broadcast(P))
 
         identity = keep.tile([P, P], F32)
         make_identity(nc, identity[:])
-
-        neg_in_col = keep.tile([P, PACK, 2], F32)
-        nc.vector.tensor_scalar_mul(out=neg_in_col[:], in0=in_col[:], scalar1=-1.0)
-        neg_hid_col = keep.tile([P, H_PASSES, PACK, 2], F32)
-        nc.vector.tensor_scalar_mul(out=neg_hid_col[:], in0=hid_col[:], scalar1=-1.0)
-        b1_col = keep.tile([P, H_PASSES, PACK], F32)
+        identity_bf = keep.tile([P, P], BF16)
+        make_identity(nc, identity_bf[:])
+        consts = {"identity": identity[:], "one": one[:]}
+        neg_hid_blk = keep.tile([P, H // P, 2], F32)
+        nc.vector.tensor_scalar_mul(out=neg_hid_blk[:], in0=hid_blk[:], scalar1=-1.0)
+        neg_out_blk = keep.tile([P, O // P, 2], F32)
+        nc.vector.tensor_scalar_mul(out=neg_out_blk[:], in0=out_blk[:], scalar1=-1.0)
+        b1_col = keep.tile([P, H // P], F32)
         nc.vector.tensor_copy(out=b1_col[:], in_=b1_bf[:])
 
-        x_words = x_sb[:].bitcast(F32).rearrange("b (p u) -> b u p", u=2)
-        xT_ps = psum.tile([P, 2, B], F32)
-        for u in range(2):
-            nc.tensor.transpose(out=xT_ps[:, u, :], in_=x_words[:, u, :], identity=identity[:])
-        x_grouped = keep.tile([P, B * PACK], BF16, align_bytes=64)
-        nc.vector.tensor_copy(
-            out=x_grouped[:].bitcast(F32).rearrange("p (b u) -> p b u", u=2),
-            in_=xT_ps[:].rearrange("p u b -> p b u"),
-        )
+        xT_ps = psum.tile([P, PACK, B], BF16)
+        for j in range(PACK):
+            nc.tensor.transpose(
+                out=xT_ps[:, j, :], in_=x_sb[:, j * P : (j + 1) * P], identity=identity_bf[:]
+            )
+        x_grouped = keep.tile([P, B, PACK], BF16, align_bytes=64)
+        nc.vector.tensor_copy(out=x_grouped[:], in_=xT_ps[:].rearrange("p j b -> p b j"))
         x_codes = keep.tile([P, B], U32, align_bytes=64)
         x_scales = keep.tile([P, B], U8, align_bytes=64)
-        nc.vector.quantize_mx(out=x_codes[:].bitcast(FP8X4), scales=x_scales[:], in_=x_grouped[:])
+        nc.vector.quantize_mx(
+            out=x_codes[:].bitcast(FP8X4),
+            scales=x_scales[:],
+            in_=x_grouped[:].rearrange("p b j -> p (b j)"),
+        )
 
-        w1_grouped = keep.tile([P, H_PASSES, PACK, P, PACK], BF16, align_bytes=64)
+        w1_grouped = keep.tile([P, H, PACK], BF16, align_bytes=64)
         w1_codes = keep.tile([P, H], U32, align_bytes=64)
         w1_scales = keep.tile([P, H], U8, align_bytes=64)
-        hid_row_xy = hid_row[:].rearrange("p (h c) -> p h c", c=2)
-        for g in range(H_PASSES):
-            for part in range(K_PASS // COLS):
-                h_cols = slice(g * K_PASS + part * COLS, g * K_PASS + (part + 1) * COLS)
-                q_range = slice(part * COLS // PACK, (part + 1) * COLS // PACK)
-                effective_weight_chunk(
-                    nc,
-                    work,
-                    w_rows=w1_sb[:, :, h_cols],
-                    row_pos=hid_row_xy[:, h_cols, :],
-                    neg_col_pos=neg_in_col[:],
-                    eff_out=w1_grouped[:, g, :, q_range, :].rearrange("p t q j -> p q j t"),
-                )
-            g_cols = slice(g * K_PASS, (g + 1) * K_PASS)
+        in_row_xy = in_row[:].rearrange("p (i c) -> p i c", c=2)
+        for chunk in range(H // COLS):
+            h_cols = slice(chunk * COLS, (chunk + 1) * COLS)
+            effective_weight_chunk(
+                nc,
+                pools,
+                consts,
+                w_rows=w1_sb[:, :, h_cols],
+                k_pos=in_row_xy,
+                neg_col_pos=neg_hid_blk[:, chunk * COL_BLOCKS : (chunk + 1) * COL_BLOCKS, :],
+                eff_out=w1_grouped[:, h_cols, :],
+                square_on_vector=(chunk % VECTOR_SQUARES_EVERY == VECTOR_SQUARES_EVERY - 1),
+            )
             nc.vector.quantize_mx(
-                out=w1_codes[:, g_cols].bitcast(FP8X4),
-                scales=w1_scales[:, g_cols],
-                in_=w1_grouped[:, g].rearrange("p t q j -> p (t q j)"),
+                out=w1_codes[:, h_cols].bitcast(FP8X4),
+                scales=w1_scales[:, h_cols],
+                in_=w1_grouped[:, h_cols, :].rearrange("p h j -> p (h j)"),
             )
 
         hid_pre = keep.tile([P, H_PASSES, B, PACK], F32)
@@ -191,24 +227,28 @@ def tile_physicalneuralnetwork_s_kernel(
             nc.vector.tensor_tensor(
                 out=hid_pre[:, g],
                 in0=hid_ps[:].rearrange("q t b -> q b t"),
-                in1=b1_col[:, g, :].unsqueeze(1).to_broadcast([P, B, PACK]),
+                in1=b1_col[:, g * PACK : (g + 1) * PACK].unsqueeze(1).to_broadcast([P, B, PACK]),
                 op=ALU.add,
             )
 
         w2_grouped = keep.tile([P, H_PASSES, O, PACK], BF16, align_bytes=64)
         w2_codes = keep.tile([P, H_PASSES, O], U32, align_bytes=64)
         w2_scales = keep.tile([P, H_PASSES, O], U8, align_bytes=64)
-        out_row_xy = out_row[:].rearrange("p (o c) -> p o c", c=2)
+        hid_row_xy = hid_row[:].rearrange("p (h c) -> p h c", c=2)
         for g in range(H_PASSES):
-            for part in range(O // COLS):
-                o_cols = slice(part * COLS, (part + 1) * COLS)
+            for chunk in range(O // COLS):
+                o_cols = slice(chunk * COLS, (chunk + 1) * COLS)
                 effective_weight_chunk(
                     nc,
-                    work,
+                    pools,
+                    consts,
                     w_rows=w2_sb[:, g, :, o_cols],
-                    row_pos=out_row_xy[:, o_cols, :],
-                    neg_col_pos=neg_hid_col[:, g],
-                    eff_out=w2_grouped[:, g, o_cols, :].rearrange("p (a i) j -> p a j i", i=4),
+                    k_pos=hid_row_xy[:, g * K_PASS : (g + 1) * K_PASS, :],
+                    neg_col_pos=neg_out_blk[:, chunk * COL_BLOCKS : (chunk + 1) * COL_BLOCKS, :],
+                    eff_out=w2_grouped[:, g, o_cols, :],
+                    square_on_vector=(
+                        (g * (O // COLS) + chunk) % VECTOR_SQUARES_EVERY == VECTOR_SQUARES_EVERY - 1
+                    ),
                 )
                 nc.vector.quantize_mx(
                     out=w2_codes[:, g, o_cols].bitcast(FP8X4),
@@ -241,7 +281,11 @@ def tile_physicalneuralnetwork_s_kernel(
                 stop=(g == H_PASSES - 1),
             )
         out_pre = keep.tile([P, O], F32)
-        nc.vector.tensor_tensor(out=out_pre[:], in0=out_ps[:], in1=b2_row[:], op=ALU.add)
         out_sb = keep.tile([P, O], F32)
-        nc.scalar.activation(out=out_sb[:], in_=out_pre[:], func=FUNC.Sigmoid)
-        nc.sync.dma_start(out=out, in_=out_sb[:])
+        for half in range(2):
+            o_cols = slice(half * O // 2, (half + 1) * O // 2)
+            nc.vector.tensor_tensor(
+                out=out_pre[:, o_cols], in0=out_ps[:, o_cols], in1=b2_row[:, o_cols], op=ALU.add
+            )
+            nc.scalar.activation(out=out_sb[:, o_cols], in_=out_pre[:, o_cols], func=FUNC.Sigmoid)
+            nc.sync.dma_start(out=out[:, o_cols], in_=out_sb[:, o_cols])

@@ -20,6 +20,7 @@ H_PASSES = H // K_PASS
 COLS = 256
 COL_BLOCKS = COLS // P
 VECTOR_SQUARES_EVERY = 4
+WEIGHT_TERMS_AHEAD = 2
 
 RHO_OVER_T = 1.68e-8 / 35e-6
 W_LIMIT = 3.0
@@ -31,230 +32,302 @@ LENGTH_SCALE = RHO_OVER_T / WIDTH_SLOPE
 FLOPS = 2 * B * I * H + 2 * B * H * O
 
 
-def effective_weight_chunk(
-    nc, pools, consts, w_rows, k_pos, neg_col_pos, eff_out, square_on_vector
-):
-    clipped = pools["work"].tile([P, PACK, COLS], BF16)
-    nc.vector.tensor_scalar(
-        out=clipped[:], in0=w_rows, scalar1=-W_LIMIT, scalar2=W_LIMIT, op0=ALU.max, op1=ALU.min
-    )
-    numer = pools["work"].tile([P, PACK, COLS], F32)
-    nc.vector.scalar_tensor_tensor(
-        out=numer[:], in0=clipped[:], scalar=BETA, in1=w_rows, op0=ALU.add, op1=ALU.mult
-    )
-
-    denom = pools["work"].tile([P, PACK, COLS], F32)
-    for u in range(COL_BLOCKS):
-        dist_x = pools["dist"].tile([P, K_PASS], F32)
-        dist_y = pools["dist"].tile([P, K_PASS], F32)
-        nc.scalar.activation(
-            out=dist_x[:], in_=k_pos[:, :, 0], func=FUNC.Abs, bias=neg_col_pos[:, u, 0:1]
-        )
-        nc.scalar.activation(
-            out=dist_y[:], in_=k_pos[:, :, 1], func=FUNC.Abs, bias=neg_col_pos[:, u, 1:2]
-        )
-        length_ps = pools["length"].tile([P, PACK, P], F32)
-        for j in range(PACK):
-            k_cols = slice(j * P, (j + 1) * P)
-            nc.tensor.matmul(
-                out=length_ps[:, j, :],
-                lhsT=dist_x[:, k_cols],
-                rhs=consts["identity"],
-                is_transpose=True,
-                start=True,
-                stop=False,
-            )
-            nc.tensor.matmul(
-                out=length_ps[:, j, :],
-                lhsT=dist_y[:, k_cols],
-                rhs=consts["identity"],
-                is_transpose=True,
-                start=False,
-                stop=True,
-            )
-        u_cols = slice(u * P, (u + 1) * P)
-        nc.vector.scalar_tensor_tensor(
-            out=denom[:, :, u_cols],
-            in0=length_ps[:],
-            scalar=LENGTH_SCALE,
-            in1=clipped[:, :, u_cols],
-            op0=ALU.mult,
-            op1=ALU.add,
-        )
-
-    rsqrt = pools["work"].tile([P, PACK, COLS], F32)
-    nc.scalar.activation(
-        out=rsqrt[:],
-        in_=denom[:],
-        func=FUNC.Abs_reciprocal_sqrt,
-        scale=1.0 / BETA,
-        bias=consts["one"],
-    )
-    first = pools["work"].tile([P, PACK, COLS], F32)
-    if square_on_vector:
-        nc.vector.scalar_tensor_tensor(
-            out=first[:], in0=numer[:], scalar=1.0 / BETA, in1=rsqrt[:], op0=ALU.mult, op1=ALU.mult
-        )
-        second = rsqrt
-    else:
-        nc.scalar.activation(
-            out=first[:], in_=rsqrt[:], func=FUNC.Square, scale=1.0 / math.sqrt(BETA)
-        )
-        second = numer
-
-    nc.vector.tensor_tensor(
-        out=eff_out.rearrange("p (a i) j -> p a j i", i=4),
-        in0=first[:].rearrange("p j (a i) -> p a j i", i=4),
-        in1=second[:].rearrange("p j (a i) -> p a j i", i=4),
-        op=ALU.mult,
-    )
-
-
 def tile_physicalneuralnetwork_s_kernel(
     tc, x, W1, b1, W2, b2, input_positions, hidden_positions, output_positions, out
 ):
     nc = tc.nc
     with ExitStack() as stack:
         keep = stack.enter_context(tc.tile_pool(name="keep", bufs=1))
-        pools = {
-            "work": stack.enter_context(tc.tile_pool(name="work", bufs=3)),
-            "dist": stack.enter_context(tc.tile_pool(name="dist", bufs=6)),
-            "length": stack.enter_context(tc.psum_pool(name="length", bufs=4)),
-        }
+        ahead = stack.enter_context(tc.tile_pool(name="ahead", bufs=WEIGHT_TERMS_AHEAD + 4))
+        work = stack.enter_context(tc.tile_pool(name="work", bufs=3))
+        dist = stack.enter_context(tc.tile_pool(name="dist", bufs=3 * COL_BLOCKS))
+        length = stack.enter_context(tc.psum_pool(name="length", bufs=2 * COL_BLOCKS))
         psum = stack.enter_context(tc.psum_pool(name="psum", bufs=1))
+        stack.enter_context(tc.manual_schedule())
+
+        identity = keep.tile([P, P], F32)
+        make_identity(nc, identity[:])
+        identity_bf = keep.tile([P, P], BF16)
+        make_identity(nc, identity_bf[:])
 
         hid_blk = keep.tile([P, H // P, 2], BF16)
         nc.scalar.dma_start(out=hid_blk[:], in_=hidden_positions.rearrange("(m r) c -> r m c", r=P))
-        out_blk = keep.tile([P, O // P, 2], BF16)
-        nc.scalar.dma_start(out=out_blk[:], in_=output_positions.rearrange("(m r) c -> r m c", r=P))
-        b1_bf = keep.tile([P, H // P], BF16)
-        with nc.allow_non_contiguous_dma(reason="1,024 bias values, one to a partition and block"):
-            nc.scalar.dma_start(out=b1_bf[:], in_=b1.rearrange("(m r) -> r m", r=P))
-
-        one = keep.tile([P, 1], F32)
-        nc.vector.memset(one[:], 1.0)
-        table_warmer = keep.tile([P, 1], F32)
-        nc.scalar.activation(out=table_warmer[:], in_=one[:], func=FUNC.Abs_reciprocal_sqrt)
-
         in_row = keep.tile([P, I * 2], BF16)
         nc.sync.dma_start(
             out=in_row[:], in_=input_positions.rearrange("i c -> (i c)").partition_broadcast(P)
         )
         w1_sb = keep.tile([P, PACK, H], BF16)
-        for half in range(2):
-            h_cols = slice(half * H // 2, (half + 1) * H // 2)
-            nc.sync.dma_start(
-                out=w1_sb[:, :, h_cols], in_=W1.rearrange("(j p) h -> p j h", p=P)[:, :, h_cols]
-            )
+        w1_view = W1.rearrange("(j p) h -> p j h", p=P)
+        nc.scalar.dma_start(out=w1_sb[:, :, : H // 2], in_=w1_view[:, :, : H // 2])
+        nc.sync.dma_start(out=w1_sb[:, :, H // 2 :], in_=w1_view[:, :, H // 2 :])
         x_sb = keep.tile([P, I], BF16)
         nc.sync.dma_start(out=x_sb[:], in_=x)
-        hid_row = keep.tile([P, H * 2], BF16)
-        nc.sync.dma_start(
-            out=hid_row[:], in_=hidden_positions.rearrange("h c -> (h c)").partition_broadcast(P)
-        )
         w2_sb = keep.tile([P, H_PASSES, PACK, O], BF16)
         for g in range(H_PASSES):
             nc.sync.dma_start(
                 out=w2_sb[:, g, :, :],
                 in_=W2[g * K_PASS : (g + 1) * K_PASS, :].rearrange("(j p) o -> p j o", p=P),
             )
+        hid_row = keep.tile([P, H * 2], BF16)
+        nc.sync.dma_start(
+            out=hid_row[:], in_=hidden_positions.rearrange("h c -> (h c)").partition_broadcast(P)
+        )
+        out_blk = keep.tile([P, O // P, 2], BF16)
+        nc.gpsimd.dma_start(out=out_blk[:], in_=output_positions.rearrange("(m r) c -> r m c", r=P))
+        b1_bf = keep.tile([P, H // P], BF16)
+        with nc.allow_non_contiguous_dma(reason="1,024 bias values, one to a partition and block"):
+            nc.gpsimd.dma_start(out=b1_bf[:], in_=b1.rearrange("(m r) -> r m", r=P))
         b2_row = keep.tile([P, O], BF16)
-        nc.sync.dma_start(out=b2_row[:], in_=b2.partition_broadcast(P))
+        nc.gpsimd.dma_start(out=b2_row[:], in_=b2.partition_broadcast(P))
 
-        identity = keep.tile([P, P], F32)
-        make_identity(nc, identity[:])
-        identity_bf = keep.tile([P, P], BF16)
-        make_identity(nc, identity_bf[:])
-        consts = {"identity": identity[:], "one": one[:]}
+        one = keep.tile([P, 1], F32)
+        nc.vector.memset(one[:], 1.0)
+        table_warmer = keep.tile([P, 1], F32)
+        nc.scalar.activation(out=table_warmer[:], in_=one[:], func=FUNC.Abs_reciprocal_sqrt)
         neg_hid_blk = keep.tile([P, H // P, 2], F32)
         nc.vector.tensor_scalar_mul(out=neg_hid_blk[:], in0=hid_blk[:], scalar1=-1.0)
-        neg_out_blk = keep.tile([P, O // P, 2], F32)
-        nc.vector.tensor_scalar_mul(out=neg_out_blk[:], in0=out_blk[:], scalar1=-1.0)
-        b1_col = keep.tile([P, H // P], F32)
-        nc.vector.tensor_copy(out=b1_col[:], in_=b1_bf[:])
 
-        xT_ps = psum.tile([P, PACK, B], BF16)
-        for j in range(PACK):
-            nc.tensor.transpose(
-                out=xT_ps[:, j, :], in_=x_sb[:, j * P : (j + 1) * P], identity=identity_bf[:]
-            )
-        x_grouped = keep.tile([P, B, PACK], BF16, align_bytes=64)
-        nc.vector.tensor_copy(out=x_grouped[:], in_=xT_ps[:].rearrange("p j b -> p b j"))
         x_codes = keep.tile([P, B], U32, align_bytes=64)
         x_scales = keep.tile([P, B], U8, align_bytes=64)
-        nc.vector.quantize_mx(
-            out=x_codes[:].bitcast(FP8X4),
-            scales=x_scales[:],
-            in_=x_grouped[:].rearrange("p b j -> p (b j)"),
-        )
-
         w1_grouped = keep.tile([P, H, PACK], BF16, align_bytes=64)
         w1_codes = keep.tile([P, H], U32, align_bytes=64)
         w1_scales = keep.tile([P, H], U8, align_bytes=64)
-        in_row_xy = in_row[:].rearrange("p (i c) -> p i c", c=2)
-        for chunk in range(H // COLS):
-            h_cols = slice(chunk * COLS, (chunk + 1) * COLS)
-            effective_weight_chunk(
-                nc,
-                pools,
-                consts,
-                w_rows=w1_sb[:, :, h_cols],
-                k_pos=in_row_xy,
-                neg_col_pos=neg_hid_blk[:, chunk * COL_BLOCKS : (chunk + 1) * COL_BLOCKS, :],
-                eff_out=w1_grouped[:, h_cols, :],
-                square_on_vector=(chunk % VECTOR_SQUARES_EVERY == VECTOR_SQUARES_EVERY - 1),
-            )
-            nc.vector.quantize_mx(
-                out=w1_codes[:, h_cols].bitcast(FP8X4),
-                scales=w1_scales[:, h_cols],
-                in_=w1_grouped[:, h_cols, :].rearrange("p h j -> p (h j)"),
-            )
-
-        hid_pre = keep.tile([P, H_PASSES, B, PACK], F32)
-        for g in range(H_PASSES):
-            hid_ps = psum.tile([P, PACK, B], F32, name="hid_ps%d" % g)
-            for t in range(PACK):
-                unit_cols = slice((g * PACK + t) * P, (g * PACK + t + 1) * P)
-                nc.tensor.matmul_mx(
-                    out=hid_ps[:, t, :],
-                    lhsT=w1_codes[:, unit_cols].bitcast(FP8X4),
-                    lhsT_scale=w1_scales[:, unit_cols],
-                    rhs=x_codes[:].bitcast(FP8X4),
-                    rhs_scale=x_scales[:],
-                    start=True,
-                    stop=True,
-                )
-            nc.vector.tensor_tensor(
-                out=hid_pre[:, g],
-                in0=hid_ps[:].rearrange("q t b -> q b t"),
-                in1=b1_col[:, g * PACK : (g + 1) * PACK].unsqueeze(1).to_broadcast([P, B, PACK]),
-                op=ALU.add,
-            )
-
         w2_grouped = keep.tile([P, H_PASSES, O, PACK], BF16, align_bytes=64)
         w2_codes = keep.tile([P, H_PASSES, O], U32, align_bytes=64)
         w2_scales = keep.tile([P, H_PASSES, O], U8, align_bytes=64)
+        neg_out_blk = keep.tile([P, O // P, 2], F32)
+
+        in_row_xy = in_row[:].rearrange("p (i c) -> p i c", c=2)
         hid_row_xy = hid_row[:].rearrange("p (h c) -> p h c", c=2)
+        chunks = []
+        for part in range(H // COLS):
+            cols = slice(part * COLS, (part + 1) * COLS)
+            chunks.append(
+                {
+                    "w_rows": w1_sb[:, :, cols],
+                    "k_pos": in_row_xy,
+                    "neg_col_pos": neg_hid_blk[:, part * COL_BLOCKS : (part + 1) * COL_BLOCKS, :],
+                    "grouped": w1_grouped[:, cols, :],
+                    "codes": w1_codes[:, cols],
+                    "scales": w1_scales[:, cols],
+                }
+            )
+        w1_chunks = len(chunks)
         for g in range(H_PASSES):
-            for chunk in range(O // COLS):
-                o_cols = slice(chunk * COLS, (chunk + 1) * COLS)
-                effective_weight_chunk(
-                    nc,
-                    pools,
-                    consts,
-                    w_rows=w2_sb[:, g, :, o_cols],
-                    k_pos=hid_row_xy[:, g * K_PASS : (g + 1) * K_PASS, :],
-                    neg_col_pos=neg_out_blk[:, chunk * COL_BLOCKS : (chunk + 1) * COL_BLOCKS, :],
-                    eff_out=w2_grouped[:, g, o_cols, :],
-                    square_on_vector=(
-                        (g * (O // COLS) + chunk) % VECTOR_SQUARES_EVERY == VECTOR_SQUARES_EVERY - 1
-                    ),
+            for part in range(O // COLS):
+                cols = slice(part * COLS, (part + 1) * COLS)
+                chunks.append(
+                    {
+                        "w_rows": w2_sb[:, g, :, cols],
+                        "k_pos": hid_row_xy[:, g * K_PASS : (g + 1) * K_PASS, :],
+                        "neg_col_pos": neg_out_blk[
+                            :, part * COL_BLOCKS : (part + 1) * COL_BLOCKS, :
+                        ],
+                        "grouped": w2_grouped[:, g, cols, :],
+                        "codes": w2_codes[:, g, cols],
+                        "scales": w2_scales[:, g, cols],
+                    }
                 )
-                nc.vector.quantize_mx(
-                    out=w2_codes[:, g, o_cols].bitcast(FP8X4),
-                    scales=w2_scales[:, g, o_cols],
-                    in_=w2_grouped[:, g, o_cols, :].rearrange("p o j -> p (o j)"),
+
+        def weight_terms(chunk):
+            clipped = ahead.tile([P, PACK, COLS], BF16, name="clipped")
+            nc.vector.tensor_scalar(
+                out=clipped[:],
+                in0=chunk["w_rows"],
+                scalar1=-W_LIMIT,
+                scalar2=W_LIMIT,
+                op0=ALU.max,
+                op1=ALU.min,
+            )
+            numer = ahead.tile([P, PACK, COLS], F32, name="numer")
+            nc.vector.scalar_tensor_tensor(
+                out=numer[:],
+                in0=clipped[:],
+                scalar=BETA,
+                in1=chunk["w_rows"],
+                op0=ALU.add,
+                op1=ALU.mult,
+            )
+            chunk["clipped"] = clipped
+            chunk["numer"] = numer
+
+        def distances(chunk):
+            chunk["dist"] = []
+            for u in range(COL_BLOCKS):
+                dist_x = dist.tile([P, K_PASS], F32, name="dist_x")
+                dist_y = dist.tile([P, K_PASS], F32, name="dist_y")
+                nc.scalar.activation(
+                    out=dist_x[:],
+                    in_=chunk["k_pos"][:, :, 0],
+                    func=FUNC.Abs,
+                    bias=chunk["neg_col_pos"][:, u, 0:1],
                 )
+                nc.scalar.activation(
+                    out=dist_y[:],
+                    in_=chunk["k_pos"][:, :, 1],
+                    func=FUNC.Abs,
+                    bias=chunk["neg_col_pos"][:, u, 1:2],
+                )
+                chunk["dist"].append((dist_x, dist_y))
+
+        def lengths(chunk):
+            chunk["length"] = []
+            for dist_x, dist_y in chunk["dist"]:
+                length_ps = length.tile([P, PACK, P], F32, name="length_ps")
+                for j in range(PACK):
+                    k_cols = slice(j * P, (j + 1) * P)
+                    nc.tensor.matmul(
+                        out=length_ps[:, j, :],
+                        lhsT=dist_x[:, k_cols],
+                        rhs=identity[:],
+                        is_transpose=True,
+                        start=True,
+                        stop=False,
+                    )
+                    nc.tensor.matmul(
+                        out=length_ps[:, j, :],
+                        lhsT=dist_y[:, k_cols],
+                        rhs=identity[:],
+                        is_transpose=True,
+                        start=False,
+                        stop=True,
+                    )
+                chunk["length"].append(length_ps)
+
+        def denominators(chunk):
+            denom = work.tile([P, PACK, COLS], F32, name="denom")
+            for u in range(COL_BLOCKS):
+                u_cols = slice(u * P, (u + 1) * P)
+                nc.vector.scalar_tensor_tensor(
+                    out=denom[:, :, u_cols],
+                    in0=chunk["length"][u][:],
+                    scalar=LENGTH_SCALE,
+                    in1=chunk["clipped"][:, :, u_cols],
+                    op0=ALU.mult,
+                    op1=ALU.add,
+                )
+            chunk["denom"] = denom
+
+        def reciprocal_roots(chunk, square_on_vector):
+            rsqrt = work.tile([P, PACK, COLS], F32, name="rsqrt")
+            nc.scalar.activation(
+                out=rsqrt[:],
+                in_=chunk["denom"][:],
+                func=FUNC.Abs_reciprocal_sqrt,
+                scale=1.0 / BETA,
+                bias=one[:],
+            )
+            chunk["rsqrt"] = rsqrt
+            if not square_on_vector:
+                recip = work.tile([P, PACK, COLS], F32, name="recip")
+                nc.scalar.activation(
+                    out=recip[:], in_=rsqrt[:], func=FUNC.Square, scale=1.0 / math.sqrt(BETA)
+                )
+                chunk["recip"] = recip
+
+        def products(chunk, square_on_vector):
+            if square_on_vector:
+                partial = work.tile([P, PACK, COLS], F32, name="partial")
+                nc.vector.scalar_tensor_tensor(
+                    out=partial[:],
+                    in0=chunk["numer"][:],
+                    scalar=1.0 / BETA,
+                    in1=chunk["rsqrt"][:],
+                    op0=ALU.mult,
+                    op1=ALU.mult,
+                )
+                factors = (partial, chunk["rsqrt"])
+            else:
+                factors = (chunk["numer"], chunk["recip"])
+            nc.vector.tensor_tensor(
+                out=chunk["grouped"].rearrange("p (a i) j -> p a j i", i=4),
+                in0=factors[0][:].rearrange("p j (a i) -> p a j i", i=4),
+                in1=factors[1][:].rearrange("p j (a i) -> p a j i", i=4),
+                op=ALU.mult,
+            )
+
+        def quantise(chunk):
+            nc.vector.quantize_mx(
+                out=chunk["codes"].bitcast(FP8X4),
+                scales=chunk["scales"],
+                in_=chunk["grouped"].rearrange("p c j -> p (c j)"),
+            )
+
+        xT_ps = psum.tile([P, PACK, B], BF16)
+        x_grouped = keep.tile([P, B, PACK], BF16, align_bytes=64)
+        b1_col = keep.tile([P, H // P], F32)
+        hid_pre = keep.tile([P, H_PASSES, B, PACK], F32)
+        hid_ps = [psum.tile([P, PACK, B], F32, name="hid_ps%d" % g) for g in range(H_PASSES)]
+
+        def transpose_x():
+            for j in range(PACK):
+                nc.tensor.transpose(
+                    out=xT_ps[:, j, :], in_=x_sb[:, j * P : (j + 1) * P], identity=identity_bf[:]
+                )
+
+        def quantise_x():
+            nc.vector.tensor_copy(out=x_grouped[:], in_=xT_ps[:].rearrange("p j b -> p b j"))
+            nc.vector.tensor_scalar_mul(out=neg_out_blk[:], in0=out_blk[:], scalar1=-1.0)
+            nc.vector.tensor_copy(out=b1_col[:], in_=b1_bf[:])
+            nc.vector.quantize_mx(
+                out=x_codes[:].bitcast(FP8X4),
+                scales=x_scales[:],
+                in_=x_grouped[:].rearrange("p b j -> p (b j)"),
+            )
+
+        def first_product():
+            for g in range(H_PASSES):
+                for t in range(PACK):
+                    unit_cols = slice((g * PACK + t) * P, (g * PACK + t + 1) * P)
+                    nc.tensor.matmul_mx(
+                        out=hid_ps[g][:, t, :],
+                        lhsT=w1_codes[:, unit_cols].bitcast(FP8X4),
+                        lhsT_scale=w1_scales[:, unit_cols],
+                        rhs=x_codes[:].bitcast(FP8X4),
+                        rhs_scale=x_scales[:],
+                        start=True,
+                        stop=True,
+                    )
+
+        def add_b1():
+            for g in range(H_PASSES):
+                nc.vector.tensor_tensor(
+                    out=hid_pre[:, g],
+                    in0=hid_ps[g][:].rearrange("q t b -> q b t"),
+                    in1=b1_col[:, g * PACK : (g + 1) * PACK]
+                    .unsqueeze(1)
+                    .to_broadcast([P, B, PACK]),
+                    op=ALU.add,
+                )
+
+        def vector_squares(c):
+            return c % VECTOR_SQUARES_EVERY == VECTOR_SQUARES_EVERY - 1
+
+        n = len(chunks)
+        for c in range(WEIGHT_TERMS_AHEAD):
+            weight_terms(chunks[c])
+        for step in range(n + 3):
+            if 0 <= step - 2 < n:
+                reciprocal_roots(chunks[step - 2], vector_squares(step - 2))
+            if step + WEIGHT_TERMS_AHEAD < n:
+                weight_terms(chunks[step + WEIGHT_TERMS_AHEAD])
+            if step < n:
+                distances(chunks[step])
+                lengths(chunks[step])
+            if 0 <= step - 1 < n:
+                denominators(chunks[step - 1])
+            if step == 1:
+                transpose_x()
+            if step == 2:
+                quantise_x()
+            if 0 <= step - 2 < n:
+                products(chunks[step - 2], vector_squares(step - 2))
+            if 0 <= step - 3 < n:
+                quantise(chunks[step - 3])
+            if step - 3 == w1_chunks - 1:
+                first_product()
+            if step - 4 == w1_chunks - 1:
+                add_b1()
 
         hid_bf = keep.tile([P, H_PASSES, B * PACK], BF16, align_bytes=64)
         hid_codes = keep.tile([P, H_PASSES, B], U32, align_bytes=64)

@@ -43,7 +43,6 @@ def tile_physicalneuralnetwork_s_kernel(
         dist = stack.enter_context(tc.tile_pool(name="dist", bufs=3 * COL_BLOCKS))
         length = stack.enter_context(tc.psum_pool(name="length", bufs=2 * COL_BLOCKS))
         psum = stack.enter_context(tc.psum_pool(name="psum", bufs=1))
-        stack.enter_context(tc.manual_schedule())
 
         identity = keep.tile([P, P], F32)
         make_identity(nc, identity[:])
@@ -60,6 +59,8 @@ def tile_physicalneuralnetwork_s_kernel(
         w1_view = W1.rearrange("(j p) h -> p j h", p=P)
         nc.scalar.dma_start(out=w1_sb[:, :, : H // 2], in_=w1_view[:, :, : H // 2])
         nc.sync.dma_start(out=w1_sb[:, :, H // 2 :], in_=w1_view[:, :, H // 2 :])
+        out_blk = keep.tile([P, O // P, 2], BF16)
+        nc.sync.dma_start(out=out_blk[:], in_=output_positions.rearrange("(m r) c -> r m c", r=P))
         x_sb = keep.tile([P, I], BF16)
         nc.sync.dma_start(out=x_sb[:], in_=x)
         w2_sb = keep.tile([P, H_PASSES, PACK, O], BF16)
@@ -72,20 +73,16 @@ def tile_physicalneuralnetwork_s_kernel(
         nc.sync.dma_start(
             out=hid_row[:], in_=hidden_positions.rearrange("h c -> (h c)").partition_broadcast(P)
         )
-        out_blk = keep.tile([P, O // P, 2], BF16)
-        nc.gpsimd.dma_start(out=out_blk[:], in_=output_positions.rearrange("(m r) c -> r m c", r=P))
         b1_bf = keep.tile([P, H // P], BF16)
         with nc.allow_non_contiguous_dma(reason="1,024 bias values, one to a partition and block"):
-            nc.gpsimd.dma_start(out=b1_bf[:], in_=b1.rearrange("(m r) -> r m", r=P))
+            nc.sync.dma_start(out=b1_bf[:], in_=b1.rearrange("(m r) -> r m", r=P))
         b2_row = keep.tile([P, O], BF16)
-        nc.gpsimd.dma_start(out=b2_row[:], in_=b2.partition_broadcast(P))
+        nc.sync.dma_start(out=b2_row[:], in_=b2.partition_broadcast(P))
 
         one = keep.tile([P, 1], F32)
         nc.vector.memset(one[:], 1.0)
         table_warmer = keep.tile([P, 1], F32)
         nc.scalar.activation(out=table_warmer[:], in_=one[:], func=FUNC.Abs_reciprocal_sqrt)
-        neg_hid_blk = keep.tile([P, H // P, 2], F32)
-        nc.vector.tensor_scalar_mul(out=neg_hid_blk[:], in0=hid_blk[:], scalar1=-1.0)
 
         x_codes = keep.tile([P, B], U32, align_bytes=64)
         x_scales = keep.tile([P, B], U8, align_bytes=64)
@@ -95,7 +92,6 @@ def tile_physicalneuralnetwork_s_kernel(
         w2_grouped = keep.tile([P, H_PASSES, O, PACK], BF16, align_bytes=64)
         w2_codes = keep.tile([P, H_PASSES, O], U32, align_bytes=64)
         w2_scales = keep.tile([P, H_PASSES, O], U8, align_bytes=64)
-        neg_out_blk = keep.tile([P, O // P, 2], F32)
 
         in_row_xy = in_row[:].rearrange("p (i c) -> p i c", c=2)
         hid_row_xy = hid_row[:].rearrange("p (h c) -> p h c", c=2)
@@ -106,10 +102,11 @@ def tile_physicalneuralnetwork_s_kernel(
                 {
                     "w_rows": w1_sb[:, :, cols],
                     "k_pos": in_row_xy,
-                    "neg_col_pos": neg_hid_blk[:, part * COL_BLOCKS : (part + 1) * COL_BLOCKS, :],
+                    "col_pos": hid_blk[:, part * COL_BLOCKS : (part + 1) * COL_BLOCKS, :],
                     "grouped": w1_grouped[:, cols, :],
                     "codes": w1_codes[:, cols],
                     "scales": w1_scales[:, cols],
+                    "length": [],
                 }
             )
         w1_chunks = len(chunks)
@@ -120,16 +117,15 @@ def tile_physicalneuralnetwork_s_kernel(
                     {
                         "w_rows": w2_sb[:, g, :, cols],
                         "k_pos": hid_row_xy[:, g * K_PASS : (g + 1) * K_PASS, :],
-                        "neg_col_pos": neg_out_blk[
-                            :, part * COL_BLOCKS : (part + 1) * COL_BLOCKS, :
-                        ],
+                        "col_pos": out_blk[:, part * COL_BLOCKS : (part + 1) * COL_BLOCKS, :],
                         "grouped": w2_grouped[:, g, cols, :],
                         "codes": w2_codes[:, g, cols],
                         "scales": w2_scales[:, g, cols],
+                        "length": [],
                     }
                 )
 
-        def weight_terms(chunk):
+        def clip_weights(chunk):
             clipped = ahead.tile([P, PACK, COLS], BF16, name="clipped")
             nc.vector.tensor_scalar(
                 out=clipped[:],
@@ -139,60 +135,51 @@ def tile_physicalneuralnetwork_s_kernel(
                 op0=ALU.max,
                 op1=ALU.min,
             )
+            chunk["clipped"] = clipped
+
+        def numerators(chunk):
             numer = ahead.tile([P, PACK, COLS], F32, name="numer")
             nc.vector.scalar_tensor_tensor(
                 out=numer[:],
-                in0=clipped[:],
+                in0=chunk["clipped"][:],
                 scalar=BETA,
                 in1=chunk["w_rows"],
                 op0=ALU.add,
                 op1=ALU.mult,
             )
-            chunk["clipped"] = clipped
             chunk["numer"] = numer
 
-        def distances(chunk):
-            chunk["dist"] = []
-            for u in range(COL_BLOCKS):
-                dist_x = dist.tile([P, K_PASS], F32, name="dist_x")
-                dist_y = dist.tile([P, K_PASS], F32, name="dist_y")
+        def lengths(chunk, u):
+            dist_x = dist.tile([P, K_PASS], F32, name="dist_x")
+            dist_y = dist.tile([P, K_PASS], F32, name="dist_y")
+            for c, dist_c in enumerate((dist_x, dist_y)):
                 nc.scalar.activation(
-                    out=dist_x[:],
-                    in_=chunk["k_pos"][:, :, 0],
+                    out=dist_c[:],
+                    in_=chunk["k_pos"][:, :, c],
                     func=FUNC.Abs,
-                    bias=chunk["neg_col_pos"][:, u, 0:1],
+                    scale=-1.0,
+                    bias=chunk["col_pos"][:, u, c : c + 1],
                 )
-                nc.scalar.activation(
-                    out=dist_y[:],
-                    in_=chunk["k_pos"][:, :, 1],
-                    func=FUNC.Abs,
-                    bias=chunk["neg_col_pos"][:, u, 1:2],
+            length_ps = length.tile([P, PACK, P], F32, name="length_ps")
+            for j in range(PACK):
+                k_cols = slice(j * P, (j + 1) * P)
+                nc.tensor.matmul(
+                    out=length_ps[:, j, :],
+                    lhsT=dist_x[:, k_cols],
+                    rhs=identity[:],
+                    is_transpose=True,
+                    start=True,
+                    stop=False,
                 )
-                chunk["dist"].append((dist_x, dist_y))
-
-        def lengths(chunk):
-            chunk["length"] = []
-            for dist_x, dist_y in chunk["dist"]:
-                length_ps = length.tile([P, PACK, P], F32, name="length_ps")
-                for j in range(PACK):
-                    k_cols = slice(j * P, (j + 1) * P)
-                    nc.tensor.matmul(
-                        out=length_ps[:, j, :],
-                        lhsT=dist_x[:, k_cols],
-                        rhs=identity[:],
-                        is_transpose=True,
-                        start=True,
-                        stop=False,
-                    )
-                    nc.tensor.matmul(
-                        out=length_ps[:, j, :],
-                        lhsT=dist_y[:, k_cols],
-                        rhs=identity[:],
-                        is_transpose=True,
-                        start=False,
-                        stop=True,
-                    )
-                chunk["length"].append(length_ps)
+                nc.tensor.matmul(
+                    out=length_ps[:, j, :],
+                    lhsT=dist_y[:, k_cols],
+                    rhs=identity[:],
+                    is_transpose=True,
+                    start=False,
+                    stop=True,
+                )
+            chunk["length"].append(length_ps)
 
         def denominators(chunk):
             denom = work.tile([P, PACK, COLS], F32, name="denom")
@@ -208,7 +195,7 @@ def tile_physicalneuralnetwork_s_kernel(
                 )
             chunk["denom"] = denom
 
-        def reciprocal_roots(chunk, square_on_vector):
+        def reciprocal_roots(chunk):
             rsqrt = work.tile([P, PACK, COLS], F32, name="rsqrt")
             nc.scalar.activation(
                 out=rsqrt[:],
@@ -218,31 +205,31 @@ def tile_physicalneuralnetwork_s_kernel(
                 bias=one[:],
             )
             chunk["rsqrt"] = rsqrt
-            if not square_on_vector:
-                recip = work.tile([P, PACK, COLS], F32, name="recip")
-                nc.scalar.activation(
-                    out=recip[:], in_=rsqrt[:], func=FUNC.Square, scale=1.0 / math.sqrt(BETA)
-                )
-                chunk["recip"] = recip
 
-        def products(chunk, square_on_vector):
-            if square_on_vector:
-                partial = work.tile([P, PACK, COLS], F32, name="partial")
-                nc.vector.scalar_tensor_tensor(
-                    out=partial[:],
-                    in0=chunk["numer"][:],
-                    scalar=1.0 / BETA,
-                    in1=chunk["rsqrt"][:],
-                    op0=ALU.mult,
-                    op1=ALU.mult,
-                )
-                factors = (partial, chunk["rsqrt"])
-            else:
-                factors = (chunk["numer"], chunk["recip"])
+        def square_on_scalar(chunk):
+            recip = work.tile([P, PACK, COLS], F32, name="recip")
+            nc.scalar.activation(
+                out=recip[:], in_=chunk["rsqrt"][:], func=FUNC.Square, scale=1.0 / math.sqrt(BETA)
+            )
+            chunk["factors"] = (chunk["numer"], recip)
+
+        def square_on_vector(chunk):
+            partial = work.tile([P, PACK, COLS], F32, name="partial")
+            nc.vector.scalar_tensor_tensor(
+                out=partial[:],
+                in0=chunk["numer"][:],
+                scalar=1.0 / BETA,
+                in1=chunk["rsqrt"][:],
+                op0=ALU.mult,
+                op1=ALU.mult,
+            )
+            chunk["factors"] = (partial, chunk["rsqrt"])
+
+        def products(chunk):
             nc.vector.tensor_tensor(
                 out=chunk["grouped"].rearrange("p (a i) j -> p a j i", i=4),
-                in0=factors[0][:].rearrange("p j (a i) -> p a j i", i=4),
-                in1=factors[1][:].rearrange("p j (a i) -> p a j i", i=4),
+                in0=chunk["factors"][0][:].rearrange("p j (a i) -> p a j i", i=4),
+                in1=chunk["factors"][1][:].rearrange("p j (a i) -> p a j i", i=4),
                 op=ALU.mult,
             )
 
@@ -265,10 +252,10 @@ def tile_physicalneuralnetwork_s_kernel(
                     out=xT_ps[:, j, :], in_=x_sb[:, j * P : (j + 1) * P], identity=identity_bf[:]
                 )
 
-        def quantise_x():
+        def group_x():
             nc.vector.tensor_copy(out=x_grouped[:], in_=xT_ps[:].rearrange("p j b -> p b j"))
-            nc.vector.tensor_scalar_mul(out=neg_out_blk[:], in0=out_blk[:], scalar1=-1.0)
-            nc.vector.tensor_copy(out=b1_col[:], in_=b1_bf[:])
+
+        def quantise_x():
             nc.vector.quantize_mx(
                 out=x_codes[:].bitcast(FP8X4),
                 scales=x_scales[:],
@@ -290,6 +277,7 @@ def tile_physicalneuralnetwork_s_kernel(
                     )
 
         def add_b1():
+            nc.vector.tensor_copy(out=b1_col[:], in_=b1_bf[:])
             for g in range(H_PASSES):
                 nc.vector.tensor_tensor(
                     out=hid_pre[:, g],
@@ -300,34 +288,47 @@ def tile_physicalneuralnetwork_s_kernel(
                     op=ALU.add,
                 )
 
+        def in_range(c):
+            return 0 <= c < len(chunks)
+
         def vector_squares(c):
             return c % VECTOR_SQUARES_EVERY == VECTOR_SQUARES_EVERY - 1
 
-        n = len(chunks)
+        for c in range(WEIGHT_TERMS_AHEAD + 1):
+            clip_weights(chunks[c])
         for c in range(WEIGHT_TERMS_AHEAD):
-            weight_terms(chunks[c])
-        for step in range(n + 3):
-            if 0 <= step - 2 < n:
-                reciprocal_roots(chunks[step - 2], vector_squares(step - 2))
-            if step + WEIGHT_TERMS_AHEAD < n:
-                weight_terms(chunks[step + WEIGHT_TERMS_AHEAD])
-            if step < n:
-                distances(chunks[step])
-                lengths(chunks[step])
-            if 0 <= step - 1 < n:
-                denominators(chunks[step - 1])
+            numerators(chunks[c])
+        for step in range(len(chunks) + 4):
+            if in_range(step - 3):
+                reciprocal_roots(chunks[step - 3])
+            if in_range(step):
+                lengths(chunks[step], 0)
+            if in_range(step - 3) and not vector_squares(step - 3):
+                square_on_scalar(chunks[step - 3])
+            if in_range(step):
+                lengths(chunks[step], 1)
             if step == 1:
                 transpose_x()
+            if in_range(step - 1):
+                denominators(chunks[step - 1])
             if step == 2:
+                group_x()
+            if in_range(step - 4):
+                quantise(chunks[step - 4])
+            if step == 3:
                 quantise_x()
-            if 0 <= step - 2 < n:
-                products(chunks[step - 2], vector_squares(step - 2))
-            if 0 <= step - 3 < n:
-                quantise(chunks[step - 3])
-            if step - 3 == w1_chunks - 1:
-                first_product()
             if step - 4 == w1_chunks - 1:
+                first_product()
+            if step - 5 == w1_chunks - 1:
                 add_b1()
+            if in_range(step - 3) and vector_squares(step - 3):
+                square_on_vector(chunks[step - 3])
+            if in_range(step + WEIGHT_TERMS_AHEAD + 1):
+                clip_weights(chunks[step + WEIGHT_TERMS_AHEAD + 1])
+            if in_range(step + WEIGHT_TERMS_AHEAD):
+                numerators(chunks[step + WEIGHT_TERMS_AHEAD])
+            if in_range(step - 3):
+                products(chunks[step - 3])
 
         hid_bf = keep.tile([P, H_PASSES, B * PACK], BF16, align_bytes=64)
         hid_codes = keep.tile([P, H_PASSES, B], U32, align_bytes=64)

@@ -51,10 +51,8 @@ def tile_physicalneuralnetwork_s_kernel(
 
         hid_blk = keep.tile([P, H // P, 2], BF16)
         nc.scalar.dma_start(out=hid_blk[:], in_=hidden_positions.rearrange("(m r) c -> r m c", r=P))
-        in_row = keep.tile([P, I * 2], BF16)
-        nc.sync.dma_start(
-            out=in_row[:], in_=input_positions.rearrange("i c -> (i c)").partition_broadcast(P)
-        )
+        in_blk = keep.tile([P, PACK, 2], BF16)
+        nc.sync.dma_start(out=in_blk[:], in_=input_positions.rearrange("(j p) c -> p j c", p=P))
         w1_sb = keep.tile([P, PACK, H], BF16)
         w1_view = W1.rearrange("(j p) h -> p j h", p=P)
         nc.scalar.dma_start(out=w1_sb[:, :, : H // 2], in_=w1_view[:, :, : H // 2])
@@ -93,7 +91,15 @@ def tile_physicalneuralnetwork_s_kernel(
         w2_codes = keep.tile([P, H_PASSES, O], U32, align_bytes=64)
         w2_scales = keep.tile([P, H_PASSES, O], U8, align_bytes=64)
 
-        in_row_xy = in_row[:].rearrange("p (i c) -> p i c", c=2)
+        in_row_ps = psum.tile([P, 2, K_PASS], BF16)
+        for c in range(2):
+            for j in range(PACK):
+                nc.tensor.transpose(
+                    out=in_row_ps[:, c, j * P : (j + 1) * P],
+                    in_=in_blk[:, j, c : c + 1].to_broadcast([P, P]),
+                    identity=identity_bf[:],
+                )
+        in_row_xy = in_row_ps[:].rearrange("p c k -> p k c")
         hid_row_xy = hid_row[:].rearrange("p (h c) -> p h c", c=2)
         chunks = []
         for part in range(H // COLS):
@@ -240,7 +246,7 @@ def tile_physicalneuralnetwork_s_kernel(
                 in_=chunk["grouped"].rearrange("p c j -> p (c j)"),
             )
 
-        xT_ps = psum.tile([P, PACK, B], BF16)
+        xT_ps = psum.tile([P, PACK, B], BF16, tag="x_then_out")
         x_grouped = keep.tile([P, B, PACK], BF16, align_bytes=64)
         b1_col = keep.tile([P, H // P], F32)
         hid_pre = keep.tile([P, H_PASSES, B, PACK], F32)
@@ -343,7 +349,7 @@ def tile_physicalneuralnetwork_s_kernel(
                 out=hid_codes[:, g, :].bitcast(FP8X4), scales=hid_scales[:, g, :], in_=hid_bf[:, g, :]
             )
 
-        out_ps = psum.tile([P, O], F32)
+        out_ps = psum.tile([P, O], F32, tag="x_then_out")
         for g in range(H_PASSES):
             nc.tensor.matmul_mx(
                 out=out_ps[:],

@@ -19,7 +19,7 @@ B, I, H, O = 128, 512, 1024, 512
 H_PASSES = H // K_PASS
 COLS = 256
 COL_BLOCKS = COLS // P
-VECTOR_SQUARES_EVERY = 4
+VECTOR_SQUARE_CHUNKS = 2
 WEIGHT_TERMS_AHEAD = 2
 
 RHO_OVER_T = 1.68e-8 / 35e-6
@@ -43,24 +43,27 @@ def tile_physicalneuralnetwork_s_kernel(
         dist = stack.enter_context(tc.tile_pool(name="dist", bufs=3 * COL_BLOCKS))
         length = stack.enter_context(tc.psum_pool(name="length", bufs=2 * COL_BLOCKS))
         psum = stack.enter_context(tc.psum_pool(name="psum", bufs=1))
+        stack.enter_context(tc.manual_schedule())
 
         identity = keep.tile([P, P], F32)
         make_identity(nc, identity[:])
         identity_bf = keep.tile([P, P], BF16)
         make_identity(nc, identity_bf[:])
 
-        hid_blk = keep.tile([P, H // P, 2], BF16)
-        nc.scalar.dma_start(out=hid_blk[:], in_=hidden_positions.rearrange("(m r) c -> r m c", r=P))
         in_blk = keep.tile([P, PACK, 2], BF16)
         nc.sync.dma_start(out=in_blk[:], in_=input_positions.rearrange("(j p) c -> p j c", p=P))
-        w1_sb = keep.tile([P, PACK, H], BF16)
+        hid_blk = keep.tile([P, H // P, 2], BF16)
+        nc.sync.dma_start(out=hid_blk[:], in_=hidden_positions.rearrange("(m r) c -> r m c", r=P))
         w1_view = W1.rearrange("(j p) h -> p j h", p=P)
-        nc.scalar.dma_start(out=w1_sb[:, :, : H // 2], in_=w1_view[:, :, : H // 2])
-        nc.sync.dma_start(out=w1_sb[:, :, H // 2 :], in_=w1_view[:, :, H // 2 :])
-        out_blk = keep.tile([P, O // P, 2], BF16)
-        nc.sync.dma_start(out=out_blk[:], in_=output_positions.rearrange("(m r) c -> r m c", r=P))
+        w1_sb = []
+        for part in range(H // COLS):
+            w1_part = keep.tile([P, PACK, COLS], BF16, name="w1_part%d" % part)
+            nc.sync.dma_start(out=w1_part[:], in_=w1_view[:, :, part * COLS : (part + 1) * COLS])
+            w1_sb.append(w1_part)
         x_sb = keep.tile([P, I], BF16)
         nc.sync.dma_start(out=x_sb[:], in_=x)
+        out_blk = keep.tile([P, O // P, 2], BF16)
+        nc.sync.dma_start(out=out_blk[:], in_=output_positions.rearrange("(m r) c -> r m c", r=P))
         w2_sb = keep.tile([P, H_PASSES, PACK, O], BF16)
         for g in range(H_PASSES):
             nc.sync.dma_start(
@@ -91,23 +94,24 @@ def tile_physicalneuralnetwork_s_kernel(
         w2_codes = keep.tile([P, H_PASSES, O], U32, align_bytes=64)
         w2_scales = keep.tile([P, H_PASSES, O], U8, align_bytes=64)
 
-        in_row_ps = psum.tile([P, 2, K_PASS], BF16)
+        in_row_ps = []
         for c in range(2):
+            spread = psum.tile([P, K_PASS], BF16, name="in_row_ps%d" % c, tag="in_then_hid%d" % c)
             for j in range(PACK):
                 nc.tensor.transpose(
-                    out=in_row_ps[:, c, j * P : (j + 1) * P],
+                    out=spread[:, j * P : (j + 1) * P],
                     in_=in_blk[:, j, c : c + 1].to_broadcast([P, P]),
                     identity=identity_bf[:],
                 )
-        in_row_xy = in_row_ps[:].rearrange("p c k -> p k c")
+            in_row_ps.append(spread)
         hid_row_xy = hid_row[:].rearrange("p (h c) -> p h c", c=2)
         chunks = []
         for part in range(H // COLS):
             cols = slice(part * COLS, (part + 1) * COLS)
             chunks.append(
                 {
-                    "w_rows": w1_sb[:, :, cols],
-                    "k_pos": in_row_xy,
+                    "w_rows": w1_sb[part][:],
+                    "k_pos": (in_row_ps[0][:], in_row_ps[1][:]),
                     "col_pos": hid_blk[:, part * COL_BLOCKS : (part + 1) * COL_BLOCKS, :],
                     "grouped": w1_grouped[:, cols, :],
                     "codes": w1_codes[:, cols],
@@ -122,7 +126,10 @@ def tile_physicalneuralnetwork_s_kernel(
                 chunks.append(
                     {
                         "w_rows": w2_sb[:, g, :, cols],
-                        "k_pos": hid_row_xy[:, g * K_PASS : (g + 1) * K_PASS, :],
+                        "k_pos": (
+                            hid_row_xy[:, g * K_PASS : (g + 1) * K_PASS, 0],
+                            hid_row_xy[:, g * K_PASS : (g + 1) * K_PASS, 1],
+                        ),
                         "col_pos": out_blk[:, part * COL_BLOCKS : (part + 1) * COL_BLOCKS, :],
                         "grouped": w2_grouped[:, g, cols, :],
                         "codes": w2_codes[:, g, cols],
@@ -161,7 +168,7 @@ def tile_physicalneuralnetwork_s_kernel(
             for c, dist_c in enumerate((dist_x, dist_y)):
                 nc.scalar.activation(
                     out=dist_c[:],
-                    in_=chunk["k_pos"][:, :, c],
+                    in_=chunk["k_pos"][c],
                     func=FUNC.Abs,
                     scale=-1.0,
                     bias=chunk["col_pos"][:, u, c : c + 1],
@@ -250,7 +257,7 @@ def tile_physicalneuralnetwork_s_kernel(
         x_grouped = keep.tile([P, B, PACK], BF16, align_bytes=64)
         b1_col = keep.tile([P, H // P], F32)
         hid_pre = keep.tile([P, H_PASSES, B, PACK], F32)
-        hid_ps = [psum.tile([P, PACK, B], F32, name="hid_ps%d" % g) for g in range(H_PASSES)]
+        hid_ps = []
 
         def transpose_x():
             for j in range(PACK):
@@ -270,6 +277,9 @@ def tile_physicalneuralnetwork_s_kernel(
 
         def first_product():
             for g in range(H_PASSES):
+                hid_ps.append(
+                    psum.tile([P, PACK, B], F32, name="hid_ps%d" % g, tag="in_then_hid%d" % g)
+                )
                 for t in range(PACK):
                     unit_cols = slice((g * PACK + t) * P, (g * PACK + t + 1) * P)
                     nc.tensor.matmul_mx(
@@ -298,11 +308,11 @@ def tile_physicalneuralnetwork_s_kernel(
             return 0 <= c < len(chunks)
 
         def vector_squares(c):
-            return c % VECTOR_SQUARES_EVERY == VECTOR_SQUARES_EVERY - 1
+            return c < VECTOR_SQUARE_CHUNKS
 
-        for c in range(WEIGHT_TERMS_AHEAD + 1):
-            clip_weights(chunks[c])
+        clip_weights(chunks[0])
         for c in range(WEIGHT_TERMS_AHEAD):
+            clip_weights(chunks[c + 1])
             numerators(chunks[c])
         for step in range(len(chunks) + 4):
             if in_range(step - 3):
@@ -315,16 +325,16 @@ def tile_physicalneuralnetwork_s_kernel(
                 lengths(chunks[step], 1)
             if step == 1:
                 transpose_x()
+            if in_range(step - 4):
+                quantise(chunks[step - 4])
+            if step - 4 == w1_chunks - 1:
+                first_product()
             if in_range(step - 1):
                 denominators(chunks[step - 1])
             if step == 2:
                 group_x()
-            if in_range(step - 4):
-                quantise(chunks[step - 4])
             if step == 3:
                 quantise_x()
-            if step - 4 == w1_chunks - 1:
-                first_product()
             if step - 5 == w1_chunks - 1:
                 add_b1()
             if in_range(step - 3) and vector_squares(step - 3):

@@ -1,4 +1,3 @@
-import math
 from contextlib import ExitStack
 
 import concourse.mybir as mybir
@@ -19,15 +18,13 @@ B, I, H, O = 128, 512, 1024, 512
 H_PASSES = H // K_PASS
 COLS = 256
 COL_BLOCKS = COLS // P
-VECTOR_SQUARE_CHUNKS = 2
-WEIGHT_TERMS_AHEAD = 2
 
 RHO_OVER_T = 1.68e-8 / 35e-6
 W_LIMIT = 3.0
 WIDTH_SLOPE = (5.0 - 0.09) / (2.0 * W_LIMIT)
 WIDTH_MID = 0.09 + W_LIMIT * WIDTH_SLOPE
 BETA = WIDTH_MID / WIDTH_SLOPE
-LENGTH_SCALE = RHO_OVER_T / WIDTH_SLOPE
+LS = RHO_OVER_T / WIDTH_SLOPE
 
 FLOPS = 2 * B * I * H + 2 * B * H * O
 
@@ -38,10 +35,10 @@ def tile_physicalneuralnetwork_s_kernel(
     nc = tc.nc
     with ExitStack() as stack:
         keep = stack.enter_context(tc.tile_pool(name="keep", bufs=1))
-        ahead = stack.enter_context(tc.tile_pool(name="ahead", bufs=WEIGHT_TERMS_AHEAD + 4))
+        ahead = stack.enter_context(tc.tile_pool(name="ahead", bufs=5))
         work = stack.enter_context(tc.tile_pool(name="work", bufs=3))
-        dist = stack.enter_context(tc.tile_pool(name="dist", bufs=3 * COL_BLOCKS))
-        length = stack.enter_context(tc.psum_pool(name="length", bufs=2 * COL_BLOCKS))
+        ps_denom = stack.enter_context(tc.psum_pool(name="ps_denom", bufs=3))
+        ps_recip = stack.enter_context(tc.psum_pool(name="ps_recip", bufs=3))
         psum = stack.enter_context(tc.psum_pool(name="psum", bufs=1))
         stack.enter_context(tc.manual_schedule())
 
@@ -50,10 +47,10 @@ def tile_physicalneuralnetwork_s_kernel(
         identity_bf = keep.tile([P, P], BF16)
         make_identity(nc, identity_bf[:])
 
-        in_blk = keep.tile([P, PACK, 2], BF16)
-        nc.sync.dma_start(out=in_blk[:], in_=input_positions.rearrange("(j p) c -> p j c", p=P))
         hid_blk = keep.tile([P, H // P, 2], BF16)
         nc.sync.dma_start(out=hid_blk[:], in_=hidden_positions.rearrange("(m r) c -> r m c", r=P))
+        in_blk = keep.tile([P, PACK, 2], BF16)
+        nc.sync.dma_start(out=in_blk[:], in_=input_positions.rearrange("(j p) c -> p j c", p=P))
         w1_view = W1.rearrange("(j p) h -> p j h", p=P)
         w1_sb = []
         for part in range(H // COLS):
@@ -62,6 +59,10 @@ def tile_physicalneuralnetwork_s_kernel(
             w1_sb.append(w1_part)
         x_sb = keep.tile([P, I], BF16)
         nc.sync.dma_start(out=x_sb[:], in_=x)
+        out_row = keep.tile([P, O * 2], BF16)
+        nc.sync.dma_start(
+            out=out_row[:], in_=output_positions.rearrange("o c -> (o c)").partition_broadcast(P)
+        )
         out_blk = keep.tile([P, O // P, 2], BF16)
         nc.sync.dma_start(out=out_blk[:], in_=output_positions.rearrange("(m r) c -> r m c", r=P))
         w2_sb = keep.tile([P, H_PASSES, PACK, O], BF16)
@@ -70,10 +71,6 @@ def tile_physicalneuralnetwork_s_kernel(
                 out=w2_sb[:, g, :, :],
                 in_=W2[g * K_PASS : (g + 1) * K_PASS, :].rearrange("(j p) o -> p j o", p=P),
             )
-        hid_row = keep.tile([P, H * 2], BF16)
-        nc.sync.dma_start(
-            out=hid_row[:], in_=hidden_positions.rearrange("h c -> (h c)").partition_broadcast(P)
-        )
         b1_bf = keep.tile([P, H // P], BF16)
         with nc.allow_non_contiguous_dma(reason="1,024 bias values, one to a partition and block"):
             nc.sync.dma_start(out=b1_bf[:], in_=b1.rearrange("(m r) -> r m", r=P))
@@ -94,52 +91,116 @@ def tile_physicalneuralnetwork_s_kernel(
         w2_codes = keep.tile([P, H_PASSES, O], U32, align_bytes=64)
         w2_scales = keep.tile([P, H_PASSES, O], U8, align_bytes=64)
 
-        in_row_ps = []
-        for c in range(2):
-            spread = psum.tile([P, K_PASS], BF16, name="in_row_ps%d" % c, tag="in_then_hid%d" % c)
-            for j in range(PACK):
+        first_x = psum.tile([P, COLS], BF16, name="first_x", tag="first_x_then_hid0")
+        rest_x = psum.tile([P, H - COLS], BF16, name="rest_x", tag="rest_x_then_hid1")
+        first_y = ps_recip.tile([P, COLS], BF16, name="first_y", tag="recip_ps")
+        rest_y = ps_recip.tile([P, H - COLS], BF16, name="rest_y", tag="recip_ps")
+
+        def spread(target, c, blocks):
+            for i, m in enumerate(blocks):
                 nc.tensor.transpose(
-                    out=spread[:, j * P : (j + 1) * P],
-                    in_=in_blk[:, j, c : c + 1].to_broadcast([P, P]),
+                    out=target[:, i * P : (i + 1) * P],
+                    in_=hid_blk[:, m, c : c + 1].to_broadcast([P, P]),
                     identity=identity_bf[:],
                 )
-            in_row_ps.append(spread)
-        hid_row_xy = hid_row[:].rearrange("p (h c) -> p h c", c=2)
+
+        spread(first_x, 0, range(COL_BLOCKS))
+        spread(first_y, 1, range(COL_BLOCKS))
+        spread(rest_y, 1, range(COL_BLOCKS, H // P))
+        spread(rest_x, 0, range(COL_BLOCKS, H // P))
+
+        in_ls = keep.tile([P, PACK, 2], F32)
+        in_2ls = keep.tile([P, PACK, 2], F32)
+        hid_ls = keep.tile([P, H // P, 2], F32)
+        hid_2ls = keep.tile([P, H // P, 2], F32)
+        hid_bias = keep.tile([P, H // P], F32)
+        out_bias = keep.tile([P, O // P], F32)
+
+        def scaled(target, source, factor):
+            nc.vector.tensor_scalar(
+                out=target, in0=source, scalar1=factor, scalar2=None, op0=ALU.mult
+            )
+
+        def column_bias(target, source):
+            nc.vector.tensor_scalar(
+                out=target, in0=source, scalar1=-LS, scalar2=BETA, op0=ALU.mult, op1=ALU.add
+            )
+
+        hid_y = keep.tile([P, H], F32)
+        out_y = keep.tile([P, O], F32)
+        out_row_xy = out_row[:].rearrange("p (o c) -> p o c", c=2)
+
+        scaled(in_ls[:], in_blk[:], LS)
+        scaled(in_2ls[:], in_blk[:], 2.0 * LS)
+        scaled(hid_y[:, 0:COLS], first_y[:], 2.0 * LS)
+
         chunks = []
         for part in range(H // COLS):
             cols = slice(part * COLS, (part + 1) * COLS)
             chunks.append(
                 {
                     "w_rows": w1_sb[part][:],
-                    "k_pos": (in_row_ps[0][:], in_row_ps[1][:]),
-                    "col_pos": hid_blk[:, part * COL_BLOCKS : (part + 1) * COL_BLOCKS, :],
+                    "col_x": first_x[:] if part == 0 else rest_x[:, (part - 1) * COLS : part * COLS],
+                    "col_y": hid_y[:, cols],
+                    "row_ls": in_ls[:],
+                    "row_2ls": in_2ls[:],
+                    "bias": hid_bias[:, part * COL_BLOCKS : (part + 1) * COL_BLOCKS],
                     "grouped": w1_grouped[:, cols, :],
                     "codes": w1_codes[:, cols],
                     "scales": w1_scales[:, cols],
-                    "length": [],
                 }
             )
         w1_chunks = len(chunks)
         for g in range(H_PASSES):
+            blocks = slice(g * PACK, (g + 1) * PACK)
             for part in range(O // COLS):
                 cols = slice(part * COLS, (part + 1) * COLS)
                 chunks.append(
                     {
                         "w_rows": w2_sb[:, g, :, cols],
-                        "k_pos": (
-                            hid_row_xy[:, g * K_PASS : (g + 1) * K_PASS, 0],
-                            hid_row_xy[:, g * K_PASS : (g + 1) * K_PASS, 1],
-                        ),
-                        "col_pos": out_blk[:, part * COL_BLOCKS : (part + 1) * COL_BLOCKS, :],
+                        "col_x": out_row_xy[:, cols, 0],
+                        "col_y": out_y[:, cols],
+                        "row_ls": hid_ls[:, blocks, :],
+                        "row_2ls": hid_2ls[:, blocks, :],
+                        "bias": out_bias[:, part * COL_BLOCKS : (part + 1) * COL_BLOCKS],
                         "grouped": w2_grouped[:, g, cols, :],
                         "codes": w2_codes[:, g, cols],
                         "scales": w2_scales[:, g, cols],
-                        "length": [],
                     }
                 )
+        n_chunks = len(chunks)
 
-        def clip_weights(chunk):
-            clipped = ahead.tile([P, PACK, COLS], BF16, name="clipped")
+        def x_distances(c, js):
+            chunk = chunks[c]
+            if "dist_x" not in chunk:
+                dist_x = work.tile([P, PACK, COLS], F32, name="dist_x")
+                chunk["dist_x"] = dist_x
+            for j in js:
+                nc.scalar.activation(
+                    out=chunk["dist_x"][:, j, :],
+                    in_=chunk["col_x"],
+                    func=FUNC.Abs,
+                    scale=-LS,
+                    bias=chunk["row_ls"][:, j, 0:1],
+                )
+
+        def y_distances(c):
+            chunk = chunks[c]
+            dist_y = work.tile([P, PACK, COLS], F32, name="dist_y")
+            for j in range(PACK):
+                nc.vector.tensor_scalar(
+                    out=dist_y[:, j, :],
+                    in0=chunk["col_y"],
+                    scalar1=chunk["row_2ls"][:, j, 1:2],
+                    scalar2=chunk["row_ls"][:, j, 1:2],
+                    op0=ALU.max,
+                    op1=ALU.subtract,
+                )
+            chunk["dist_y"] = dist_y
+
+        def clip_weights(c):
+            chunk = chunks[c]
+            clipped = ahead.tile([P, PACK, COLS], F32, name="clipped")
             nc.vector.tensor_scalar(
                 out=clipped[:],
                 in0=chunk["w_rows"],
@@ -150,7 +211,8 @@ def tile_physicalneuralnetwork_s_kernel(
             )
             chunk["clipped"] = clipped
 
-        def numerators(chunk):
+        def numerators(c):
+            chunk = chunks[c]
             numer = ahead.tile([P, PACK, COLS], F32, name="numer")
             nc.vector.scalar_tensor_tensor(
                 out=numer[:],
@@ -162,111 +224,82 @@ def tile_physicalneuralnetwork_s_kernel(
             )
             chunk["numer"] = numer
 
-        def lengths(chunk, u):
-            dist_x = dist.tile([P, K_PASS], F32, name="dist_x")
-            dist_y = dist.tile([P, K_PASS], F32, name="dist_y")
-            for c, dist_c in enumerate((dist_x, dist_y)):
-                nc.scalar.activation(
-                    out=dist_c[:],
-                    in_=chunk["k_pos"][c],
-                    func=FUNC.Abs,
-                    scale=-1.0,
-                    bias=chunk["col_pos"][:, u, c : c + 1],
-                )
-            length_ps = length.tile([P, PACK, P], F32, name="length_ps")
+        def denominators(c, u):
+            chunk = chunks[c]
+            cols = slice(u * P, (u + 1) * P)
+            denom_ps = ps_denom.tile([P, PACK, P], F32, name="denom_ps")
+            terms = (chunk["clipped"], chunk["dist_y"], chunk["dist_x"])
             for j in range(PACK):
-                k_cols = slice(j * P, (j + 1) * P)
-                nc.tensor.matmul(
-                    out=length_ps[:, j, :],
-                    lhsT=dist_x[:, k_cols],
-                    rhs=identity[:],
-                    is_transpose=True,
-                    start=True,
-                    stop=False,
-                )
-                nc.tensor.matmul(
-                    out=length_ps[:, j, :],
-                    lhsT=dist_y[:, k_cols],
-                    rhs=identity[:],
-                    is_transpose=True,
-                    start=False,
-                    stop=True,
-                )
-            chunk["length"].append(length_ps)
+                for i, term in enumerate(terms):
+                    nc.tensor.matmul(
+                        out=denom_ps[:, j, :],
+                        lhsT=term[:, j, cols],
+                        rhs=identity[:],
+                        is_transpose=True,
+                        start=(i == 0),
+                        stop=(i == len(terms) - 1),
+                    )
+            chunk["denom", u] = denom_ps
 
-        def denominators(chunk):
-            denom = work.tile([P, PACK, COLS], F32, name="denom")
-            for u in range(COL_BLOCKS):
-                u_cols = slice(u * P, (u + 1) * P)
-                nc.vector.scalar_tensor_tensor(
-                    out=denom[:, :, u_cols],
-                    in0=chunk["length"][u][:],
-                    scalar=LENGTH_SCALE,
-                    in1=chunk["clipped"][:, :, u_cols],
-                    op0=ALU.mult,
-                    op1=ALU.add,
-                )
-            chunk["denom"] = denom
-
-        def reciprocal_roots(chunk):
-            rsqrt = work.tile([P, PACK, COLS], F32, name="rsqrt")
+        def roots(c, u):
+            chunk = chunks[c]
+            root = work.tile([P, PACK, P], F32, name="root")
             nc.scalar.activation(
-                out=rsqrt[:],
-                in_=chunk["denom"][:],
+                out=root[:],
+                in_=chunk["denom", u][:],
                 func=FUNC.Abs_reciprocal_sqrt,
-                scale=1.0 / BETA,
-                bias=one[:],
+                bias=chunk["bias"][:, u : u + 1],
             )
-            chunk["rsqrt"] = rsqrt
+            chunk["root", u] = root
 
-        def square_on_scalar(chunk):
-            recip = work.tile([P, PACK, COLS], F32, name="recip")
-            nc.scalar.activation(
-                out=recip[:], in_=chunk["rsqrt"][:], func=FUNC.Square, scale=1.0 / math.sqrt(BETA)
-            )
-            chunk["factors"] = (chunk["numer"], recip)
+        def squares(c, u):
+            chunk = chunks[c]
+            recip = work.tile([P, PACK, P], F32, name="recip")
+            nc.scalar.activation(out=recip[:], in_=chunk["root", u][:], func=FUNC.Square)
+            chunk["recip", u] = recip
 
-        def square_on_vector(chunk):
-            partial = work.tile([P, PACK, COLS], F32, name="partial")
-            nc.vector.scalar_tensor_tensor(
-                out=partial[:],
-                in0=chunk["numer"][:],
-                scalar=1.0 / BETA,
-                in1=chunk["rsqrt"][:],
-                op0=ALU.mult,
-                op1=ALU.mult,
-            )
-            chunk["factors"] = (partial, chunk["rsqrt"])
+        def turn_back(c, u):
+            chunk = chunks[c]
+            recip_ps = ps_recip.tile([P, PACK, P], F32, name="recip_ps", tag="recip_ps")
+            for j in range(PACK):
+                nc.tensor.transpose(
+                    out=recip_ps[:, j, :], in_=chunk["recip", u][:, j, :], identity=identity[:]
+                )
+            chunk["recip_ps", u] = recip_ps
 
-        def products(chunk):
+        def products(c, u):
+            chunk = chunks[c]
+            cols = slice(u * P, (u + 1) * P)
             nc.vector.tensor_tensor(
-                out=chunk["grouped"].rearrange("p (a i) j -> p a j i", i=4),
-                in0=chunk["factors"][0][:].rearrange("p j (a i) -> p a j i", i=4),
-                in1=chunk["factors"][1][:].rearrange("p j (a i) -> p a j i", i=4),
+                out=chunk["grouped"][:, cols, :].rearrange("p (a i) j -> p a j i", i=4),
+                in0=chunk["recip_ps", u][:].rearrange("p j (a i) -> p a j i", i=4),
+                in1=chunk["numer"][:, :, cols].rearrange("p j (a i) -> p a j i", i=4),
                 op=ALU.mult,
             )
 
-        def quantise(chunk):
+        def quantise(c):
+            chunk = chunks[c]
             nc.vector.quantize_mx(
                 out=chunk["codes"].bitcast(FP8X4),
                 scales=chunk["scales"],
                 in_=chunk["grouped"].rearrange("p c j -> p (c j)"),
             )
 
-        xT_ps = psum.tile([P, PACK, B], BF16, tag="x_then_out")
         x_grouped = keep.tile([P, B, PACK], BF16, align_bytes=64)
         b1_col = keep.tile([P, H // P], F32)
         hid_pre = keep.tile([P, H_PASSES, B, PACK], F32)
         hid_ps = []
+        xT = []
 
         def transpose_x():
+            xT.append(ps_recip.tile([P, PACK, B], BF16, name="xT_ps", tag="recip_ps"))
             for j in range(PACK):
                 nc.tensor.transpose(
-                    out=xT_ps[:, j, :], in_=x_sb[:, j * P : (j + 1) * P], identity=identity_bf[:]
+                    out=xT[0][:, j, :], in_=x_sb[:, j * P : (j + 1) * P], identity=identity_bf[:]
                 )
 
         def group_x():
-            nc.vector.tensor_copy(out=x_grouped[:], in_=xT_ps[:].rearrange("p j b -> p b j"))
+            nc.vector.tensor_copy(out=x_grouped[:], in_=xT[0][:].rearrange("p j b -> p b j"))
 
         def quantise_x():
             nc.vector.quantize_mx(
@@ -276,10 +309,9 @@ def tile_physicalneuralnetwork_s_kernel(
             )
 
         def first_product():
+            tags = ("first_x_then_hid0", "rest_x_then_hid1")
             for g in range(H_PASSES):
-                hid_ps.append(
-                    psum.tile([P, PACK, B], F32, name="hid_ps%d" % g, tag="in_then_hid%d" % g)
-                )
+                hid_ps.append(psum.tile([P, PACK, B], F32, name="hid_ps%d" % g, tag=tags[g]))
                 for t in range(PACK):
                     unit_cols = slice((g * PACK + t) * P, (g * PACK + t + 1) * P)
                     nc.tensor.matmul_mx(
@@ -304,47 +336,63 @@ def tile_physicalneuralnetwork_s_kernel(
                     op=ALU.add,
                 )
 
-        def in_range(c):
-            return 0 <= c < len(chunks)
-
-        def vector_squares(c):
-            return c < VECTOR_SQUARE_CHUNKS
-
-        clip_weights(chunks[0])
-        for c in range(WEIGHT_TERMS_AHEAD):
-            clip_weights(chunks[c + 1])
-            numerators(chunks[c])
-        for step in range(len(chunks) + 4):
-            if in_range(step - 3):
-                reciprocal_roots(chunks[step - 3])
-            if in_range(step):
-                lengths(chunks[step], 0)
-            if in_range(step - 3) and not vector_squares(step - 3):
-                square_on_scalar(chunks[step - 3])
-            if in_range(step):
-                lengths(chunks[step], 1)
-            if step == 1:
+        x_distances(0, range(PACK))
+        y_distances(0)
+        scaled(hid_y[:, COLS:H], rest_y[:], 2.0 * LS)
+        column_bias(hid_bias[:], hid_blk[:, :, 1])
+        clip_weights(0)
+        y_distances(1)
+        x_distances(1, range(PACK))
+        clip_weights(1)
+        numerators(0)
+        denominators(0, 0)
+        denominators(0, 1)
+        for c in range(n_chunks + 2):
+            more = c + 2 < n_chunks
+            if c < n_chunks:
+                roots(c, 0)
+                if more:
+                    x_distances(c + 2, (0, 1))
+                roots(c, 1)
+                squares(c, 0)
+                if more:
+                    x_distances(c + 2, (2, 3))
+                squares(c, 1)
+            if c + 1 < n_chunks:
+                denominators(c + 1, 0)
+            if c < n_chunks:
+                turn_back(c, 0)
+            if c + 1 < n_chunks:
+                denominators(c + 1, 1)
+            if c < n_chunks:
+                turn_back(c, 1)
+            if c == 1:
                 transpose_x()
-            if in_range(step - 4):
-                quantise(chunks[step - 4])
-            if step - 4 == w1_chunks - 1:
-                first_product()
-            if in_range(step - 1):
-                denominators(chunks[step - 1])
-            if step == 2:
+            if 0 <= c - 2 < n_chunks:
+                quantise(c - 2)
+                if c - 2 == w1_chunks - 1:
+                    first_product()
+            if 0 <= c - 1 < n_chunks:
+                products(c - 1, 0)
+            if more:
+                y_distances(c + 2)
+            if 0 <= c - 1 < n_chunks:
+                products(c - 1, 1)
+            if more:
+                clip_weights(c + 2)
+            if c + 1 < n_chunks:
+                numerators(c + 1)
+            if c == 1:
+                scaled(hid_ls[:], hid_blk[:], LS)
+                scaled(hid_2ls[:], hid_blk[:], 2.0 * LS)
+                scaled(out_y[:], out_row_xy[:, :, 1], 2.0 * LS)
+                column_bias(out_bias[:], out_blk[:, :, 1])
+            if c == 2:
                 group_x()
-            if step == 3:
+            if c == 3:
                 quantise_x()
-            if step - 5 == w1_chunks - 1:
+            if c - 3 == w1_chunks - 1:
                 add_b1()
-            if in_range(step - 3) and vector_squares(step - 3):
-                square_on_vector(chunks[step - 3])
-            if in_range(step + WEIGHT_TERMS_AHEAD + 1):
-                clip_weights(chunks[step + WEIGHT_TERMS_AHEAD + 1])
-            if in_range(step + WEIGHT_TERMS_AHEAD):
-                numerators(chunks[step + WEIGHT_TERMS_AHEAD])
-            if in_range(step - 3):
-                products(chunks[step - 3])
 
         hid_bf = keep.tile([P, H_PASSES, B * PACK], BF16, align_bytes=64)
         hid_codes = keep.tile([P, H_PASSES, B], U32, align_bytes=64)
@@ -359,23 +407,26 @@ def tile_physicalneuralnetwork_s_kernel(
                 out=hid_codes[:, g, :].bitcast(FP8X4), scales=hid_scales[:, g, :], in_=hid_bf[:, g, :]
             )
 
-        out_ps = psum.tile([P, O], F32, tag="x_then_out")
-        for g in range(H_PASSES):
-            nc.tensor.matmul_mx(
-                out=out_ps[:],
-                lhsT=hid_codes[:, g, :].bitcast(FP8X4),
-                lhsT_scale=hid_scales[:, g, :],
-                rhs=w2_codes[:, g, :].bitcast(FP8X4),
-                rhs_scale=w2_scales[:, g, :],
-                start=(g == 0),
-                stop=(g == H_PASSES - 1),
-            )
         out_pre = keep.tile([P, O], F32)
         out_sb = keep.tile([P, O], F32)
+        HALF = O // 2
+        halves = [ps_denom.tile([P, HALF], F32, name="out_ps%d" % h, tag="denom_ps") for h in range(2)]
         for half in range(2):
-            o_cols = slice(half * O // 2, (half + 1) * O // 2)
+            o_cols = slice(half * HALF, (half + 1) * HALF)
+            for g in range(H_PASSES):
+                nc.tensor.matmul_mx(
+                    out=halves[half][:],
+                    lhsT=hid_codes[:, g, :].bitcast(FP8X4),
+                    lhsT_scale=hid_scales[:, g, :],
+                    rhs=w2_codes[:, g, o_cols].bitcast(FP8X4),
+                    rhs_scale=w2_scales[:, g, o_cols],
+                    start=(g == 0),
+                    stop=(g == H_PASSES - 1),
+                )
+        for half in range(2):
+            o_cols = slice(half * HALF, (half + 1) * HALF)
             nc.vector.tensor_tensor(
-                out=out_pre[:, o_cols], in0=out_ps[:, o_cols], in1=b2_row[:, o_cols], op=ALU.add
+                out=out_pre[:, o_cols], in0=halves[half][:], in1=b2_row[:, o_cols], op=ALU.add
             )
             nc.scalar.activation(out=out_sb[:, o_cols], in_=out_pre[:, o_cols], func=FUNC.Sigmoid)
             nc.sync.dma_start(out=out[:, o_cols], in_=out_sb[:, o_cols])

@@ -299,7 +299,7 @@ def tile_physicalneuralnetwork_s_kernel(
                 )
 
         def group_x():
-            nc.vector.tensor_copy(out=x_grouped[:], in_=xT[0][:].rearrange("p j b -> p b j"))
+            nc.scalar.copy(out=x_grouped[:], in_=xT[0][:].rearrange("p j b -> p b j"))
 
         def quantise_x():
             nc.vector.quantize_mx(
@@ -337,38 +337,36 @@ def tile_physicalneuralnetwork_s_kernel(
                 )
 
         x_distances(0, range(PACK))
+        nc.scalar.activation(out=hid_y[:, COLS:H], in_=rest_y[:], func=FUNC.Copy, scale=2.0 * LS)
         y_distances(0)
-        scaled(hid_y[:, COLS:H], rest_y[:], 2.0 * LS)
-        column_bias(hid_bias[:], hid_blk[:, :, 1])
         clip_weights(0)
+        column_bias(hid_bias[:], hid_blk[:, :, 1])
+        numerators(0)
         y_distances(1)
         x_distances(1, range(PACK))
         clip_weights(1)
-        numerators(0)
         denominators(0, 0)
         denominators(0, 1)
-        for c in range(n_chunks + 2):
+        for c in range(n_chunks + 1):
             more = c + 2 < n_chunks
             if c < n_chunks:
                 roots(c, 0)
                 if more:
                     x_distances(c + 2, (0, 1))
-                roots(c, 1)
                 squares(c, 0)
+                roots(c, 1)
                 if more:
                     x_distances(c + 2, (2, 3))
                 squares(c, 1)
             if c + 1 < n_chunks:
                 denominators(c + 1, 0)
-            if c < n_chunks:
-                turn_back(c, 0)
-            if c + 1 < n_chunks:
                 denominators(c + 1, 1)
             if c < n_chunks:
+                turn_back(c, 0)
                 turn_back(c, 1)
             if c == 1:
                 transpose_x()
-            if 0 <= c - 2 < n_chunks:
+            if 0 <= c - 2 < n_chunks - 1:
                 quantise(c - 2)
                 if c - 2 == w1_chunks - 1:
                     first_product()
@@ -403,9 +401,12 @@ def tile_physicalneuralnetwork_s_kernel(
                 in_=hid_pre[:, g].rearrange("q b t -> q (b t)"),
                 func=FUNC.Sigmoid,
             )
+        for g in range(H_PASSES):
             nc.vector.quantize_mx(
                 out=hid_codes[:, g, :].bitcast(FP8X4), scales=hid_scales[:, g, :], in_=hid_bf[:, g, :]
             )
+
+        quantise(n_chunks - 1)
 
         out_pre = keep.tile([P, O], F32)
         out_sb = keep.tile([P, O], F32)

@@ -18,6 +18,10 @@ B, I, H, O = 128, 512, 1024, 512
 H_PASSES = H // K_PASS
 COLS = 256
 COL_BLOCKS = COLS // P
+CLOCK_COLS = 32
+TURNED = (0, 1, 2, 3, 4, 5, 6, 7)
+Y_ON_SCALAR = ()
+VECTOR_SQUARES = ()
 
 RHO_OVER_T = 1.68e-8 / 35e-6
 W_LIMIT = 3.0
@@ -47,21 +51,30 @@ def tile_physicalneuralnetwork_s_kernel(
         identity_bf = keep.tile([P, P], BF16)
         make_identity(nc, identity_bf[:])
 
-        hid_blk = keep.tile([P, H // P, 2], BF16)
-        nc.sync.dma_start(out=hid_blk[:], in_=hidden_positions.rearrange("(m r) c -> r m c", r=P))
         in_blk = keep.tile([P, PACK, 2], BF16)
         nc.sync.dma_start(out=in_blk[:], in_=input_positions.rearrange("(j p) c -> p j c", p=P))
+        hid_blk = keep.tile([P, H // P, 2], BF16)
+        nc.sync.dma_start(out=hid_blk[:], in_=hidden_positions.rearrange("(m r) c -> r m c", r=P))
         w1_view = W1.rearrange("(j p) h -> p j h", p=P)
         w1_sb = []
         for part in range(H // COLS):
             w1_part = keep.tile([P, PACK, COLS], BF16, name="w1_part%d" % part)
             nc.sync.dma_start(out=w1_part[:], in_=w1_view[:, :, part * COLS : (part + 1) * COLS])
             w1_sb.append(w1_part)
+            if part == 1:
+                hid_row = keep.tile([P, H // 2, 2], BF16)
+                nc.sync.dma_start(
+                    out=hid_row[:].rearrange("p h c -> p (h c)"),
+                    in_=hidden_positions[H // 2 :, :]
+                    .rearrange("h c -> (h c)")
+                    .partition_broadcast(P),
+                )
         x_sb = keep.tile([P, I], BF16)
         nc.sync.dma_start(out=x_sb[:], in_=x)
-        out_row = keep.tile([P, O * 2], BF16)
+        out_row = keep.tile([P, O, 2], BF16)
         nc.sync.dma_start(
-            out=out_row[:], in_=output_positions.rearrange("o c -> (o c)").partition_broadcast(P)
+            out=out_row[:].rearrange("p o c -> p (o c)"),
+            in_=output_positions.rearrange("o c -> (o c)").partition_broadcast(P),
         )
         out_blk = keep.tile([P, O // P, 2], BF16)
         nc.sync.dma_start(out=out_blk[:], in_=output_positions.rearrange("(m r) c -> r m c", r=P))
@@ -91,116 +104,150 @@ def tile_physicalneuralnetwork_s_kernel(
         w2_codes = keep.tile([P, H_PASSES, O], U32, align_bytes=64)
         w2_scales = keep.tile([P, H_PASSES, O], U8, align_bytes=64)
 
-        first_x = psum.tile([P, COLS], BF16, name="first_x", tag="first_x_then_hid0")
-        rest_x = psum.tile([P, H - COLS], BF16, name="rest_x", tag="rest_x_then_hid1")
-        first_y = ps_recip.tile([P, COLS], BF16, name="first_y", tag="recip_ps")
-        rest_y = ps_recip.tile([P, H - COLS], BF16, name="rest_y", tag="recip_ps")
+        first_x = psum.tile([P, COLS], BF16, name="first_x", tag="first_x_then_hid")
+        first_y = psum.tile([P, COLS], BF16, name="first_y", tag="first_y_then_x")
+        second_xy = ps_recip.tile([P, 2, COLS], BF16, name="second_xy", tag="recip_ps")
 
-        def spread(target, c, blocks):
-            for i, m in enumerate(blocks):
+        def spread(target, chunk, c):
+            for u in range(COL_BLOCKS):
+                m = chunk * COL_BLOCKS + u
                 nc.tensor.transpose(
-                    out=target[:, i * P : (i + 1) * P],
+                    out=target[:, u * P : (u + 1) * P],
                     in_=hid_blk[:, m, c : c + 1].to_broadcast([P, P]),
                     identity=identity_bf[:],
                 )
 
-        spread(first_x, 0, range(COL_BLOCKS))
-        spread(first_y, 1, range(COL_BLOCKS))
-        spread(rest_y, 1, range(COL_BLOCKS, H // P))
-        spread(rest_x, 0, range(COL_BLOCKS, H // P))
+        def raise_clock(target, width):
+            nc.tensor.matmul(
+                out=target, lhsT=identity[:], rhs=identity[:, :width], start=True, stop=True
+            )
+
+        clock_ps = ps_denom.tile([P, PACK, P], F32, name="clock_ps", tag="sum_ps")
+        for j in range(2):
+            raise_clock(clock_ps[:, j, :], P)
+        spread(first_x[:], 0, 0)
+        spread(first_y[:], 0, 1)
+        spread(second_xy[:, 1, :], 1, 1)
+        spread(second_xy[:, 0, :], 1, 0)
+        w1_chunks = H // COLS
 
         in_ls = keep.tile([P, PACK, 2], F32)
         in_2ls = keep.tile([P, PACK, 2], F32)
         hid_ls = keep.tile([P, H // P, 2], F32)
         hid_2ls = keep.tile([P, H // P, 2], F32)
         hid_bias = keep.tile([P, H // P], F32)
+        out_ls = keep.tile([P, O // P, 2], F32)
+        out_2ls = keep.tile([P, O // P, 2], F32)
         out_bias = keep.tile([P, O // P], F32)
+        beta = keep.tile([P, 1], F32)
 
         def scaled(target, source, factor):
             nc.vector.tensor_scalar(
                 out=target, in0=source, scalar1=factor, scalar2=None, op0=ALU.mult
             )
 
-        def column_bias(target, source):
+        def y_bias(target, source):
             nc.vector.tensor_scalar(
                 out=target, in0=source, scalar1=-LS, scalar2=BETA, op0=ALU.mult, op1=ALU.add
             )
 
-        hid_y = keep.tile([P, H], F32)
-        out_y = keep.tile([P, O], F32)
-        out_row_xy = out_row[:].rearrange("p (o c) -> p o c", c=2)
-
-        scaled(in_ls[:], in_blk[:], LS)
-        scaled(in_2ls[:], in_blk[:], 2.0 * LS)
-        scaled(hid_y[:, 0:COLS], first_y[:], 2.0 * LS)
+        hid_2ls_row = keep.tile([P, H], F32)
+        out_2ls_row = keep.tile([P, O], F32)
 
         chunks = []
-        for part in range(H // COLS):
+        for part in range(w1_chunks):
             cols = slice(part * COLS, (part + 1) * COLS)
-            chunks.append(
-                {
-                    "w_rows": w1_sb[part][:],
-                    "col_x": first_x[:] if part == 0 else rest_x[:, (part - 1) * COLS : part * COLS],
-                    "col_y": hid_y[:, cols],
-                    "row_ls": in_ls[:],
-                    "row_2ls": in_2ls[:],
-                    "bias": hid_bias[:, part * COL_BLOCKS : (part + 1) * COL_BLOCKS],
-                    "grouped": w1_grouped[:, cols, :],
-                    "codes": w1_codes[:, cols],
-                    "scales": w1_scales[:, cols],
-                }
-            )
-        w1_chunks = len(chunks)
+            blocks = slice(part * COL_BLOCKS, (part + 1) * COL_BLOCKS)
+            chunk = {
+                "w_rows": w1_sb[part][:],
+                "grouped": w1_grouped[:, cols, :],
+                "codes": w1_codes[:, cols],
+                "scales": w1_scales[:, cols],
+            }
+            if part == 0:
+                chunk["free_x"] = first_x[:]
+            elif part == 1:
+                chunk["free_x"] = second_xy[:, 0, :]
+            else:
+                chunk["free_x"] = hid_row[:, (part - 2) * COLS : (part - 1) * COLS, 0]
+            chunk["free_2ls_y"] = hid_2ls_row[:, cols]
+            chunk["part_ls"] = in_ls[:]
+            chunk["part_2ls"] = in_2ls[:]
+            chunk["bias"] = hid_bias[:, blocks]
+            chunks.append(chunk)
         for g in range(H_PASSES):
-            blocks = slice(g * PACK, (g + 1) * PACK)
             for part in range(O // COLS):
                 cols = slice(part * COLS, (part + 1) * COLS)
-                chunks.append(
-                    {
-                        "w_rows": w2_sb[:, g, :, cols],
-                        "col_x": out_row_xy[:, cols, 0],
-                        "col_y": out_y[:, cols],
-                        "row_ls": hid_ls[:, blocks, :],
-                        "row_2ls": hid_2ls[:, blocks, :],
-                        "bias": out_bias[:, part * COL_BLOCKS : (part + 1) * COL_BLOCKS],
-                        "grouped": w2_grouped[:, g, cols, :],
-                        "codes": w2_codes[:, g, cols],
-                        "scales": w2_scales[:, g, cols],
-                    }
-                )
+                blocks = slice(part * COL_BLOCKS, (part + 1) * COL_BLOCKS)
+                k_blocks = slice(g * PACK, (g + 1) * PACK)
+                k_rows = slice(g * K_PASS, (g + 1) * K_PASS)
+                chunk = {
+                    "w_rows": w2_sb[:, g, :, cols],
+                    "grouped": w2_grouped[:, g, cols, :],
+                    "codes": w2_codes[:, g, cols],
+                    "scales": w2_scales[:, g, cols],
+                }
+                if len(chunks) in TURNED:
+                    chunk["free_x"] = out_row[:, cols, 0]
+                    chunk["free_2ls_y"] = out_2ls_row[:, cols]
+                    chunk["part_ls"] = hid_ls[:, k_blocks, :]
+                    chunk["part_2ls"] = hid_2ls[:, k_blocks, :]
+                    chunk["bias"] = out_bias[:, blocks]
+                else:
+                    chunk["free_x"] = hid_row[:, :, 0]
+                    chunk["free_y"] = hid_row[:, :, 1]
+                    chunk["free_2ls_y"] = hid_2ls_row[:, k_rows]
+                    chunk["part_ls"] = out_ls[:, blocks, :]
+                    chunk["part_2ls"] = out_2ls[:, blocks, :]
+                    chunk["bias"] = hid_bias[:, k_blocks]
+                chunks.append(chunk)
         n_chunks = len(chunks)
 
-        def x_distances(c, js):
+        def abs_distances(c, i, coordinate, free, target):
+            nc.scalar.activation(
+                out=target,
+                in_=free,
+                func=FUNC.Abs,
+                scale=-LS,
+                bias=chunks[c]["part_ls"][:, i, coordinate : coordinate + 1],
+            )
+
+        def distance_tile(c, name):
             chunk = chunks[c]
-            if "dist_x" not in chunk:
-                dist_x = work.tile([P, PACK, COLS], F32, name="dist_x")
-                chunk["dist_x"] = dist_x
-            for j in js:
-                nc.scalar.activation(
-                    out=chunk["dist_x"][:, j, :],
-                    in_=chunk["col_x"],
-                    func=FUNC.Abs,
-                    scale=-LS,
-                    bias=chunk["row_ls"][:, j, 0:1],
-                )
+            if name not in chunk:
+                blocks = PACK if c in TURNED else COL_BLOCKS
+                tile = work.tile([P, blocks, PACK * COLS // blocks], F32, name=name)
+                chunk[name] = tile
+            return chunk[name]
+
+        def x_distances(c, half):
+            dist_x = distance_tile(c, "dist_x")
+            n = (PACK if c in TURNED else COL_BLOCKS) // 2
+            for i in range(half * n, (half + 1) * n):
+                abs_distances(c, i, 0, chunks[c]["free_x"], dist_x[:, i, :])
+                if c in Y_ON_SCALAR:
+                    dist_y = distance_tile(c, "dist_y")
+                    abs_distances(c, i, 1, chunks[c]["free_y"], dist_y[:, i, :])
 
         def y_distances(c):
+            if c in Y_ON_SCALAR:
+                return
             chunk = chunks[c]
-            dist_y = work.tile([P, PACK, COLS], F32, name="dist_y")
-            for j in range(PACK):
+            dist_y = distance_tile(c, "dist_y")
+            for i in range(PACK if c in TURNED else COL_BLOCKS):
                 nc.vector.tensor_scalar(
-                    out=dist_y[:, j, :],
-                    in0=chunk["col_y"],
-                    scalar1=chunk["row_2ls"][:, j, 1:2],
-                    scalar2=chunk["row_ls"][:, j, 1:2],
+                    out=dist_y[:, i, :],
+                    in0=chunk["free_2ls_y"],
+                    scalar1=chunk["part_2ls"][:, i, 1:2],
+                    scalar2=chunk["part_ls"][:, i, 1:2],
                     op0=ALU.max,
                     op1=ALU.subtract,
                 )
-            chunk["dist_y"] = dist_y
 
         def clip_weights(c):
             chunk = chunks[c]
-            clipped = ahead.tile([P, PACK, COLS], F32, name="clipped")
+            dtype, name = (F32, "clipped") if c in TURNED else (BF16, "clipped_bf")
+            clipped = ahead.tile([P, PACK, COLS], dtype, name=name)
             nc.vector.tensor_scalar(
                 out=clipped[:],
                 in0=chunk["w_rows"],
@@ -224,56 +271,117 @@ def tile_physicalneuralnetwork_s_kernel(
             )
             chunk["numer"] = numer
 
-        def denominators(c, u):
+        def turned_sum(target, terms):
+            for i, term in enumerate(terms):
+                nc.tensor.matmul(
+                    out=target,
+                    lhsT=term,
+                    rhs=identity[:],
+                    is_transpose=True,
+                    start=(i == 0),
+                    stop=(i == len(terms) - 1),
+                )
+
+        def turn(c, u):
             chunk = chunks[c]
             cols = slice(u * P, (u + 1) * P)
-            denom_ps = ps_denom.tile([P, PACK, P], F32, name="denom_ps")
-            terms = (chunk["clipped"], chunk["dist_y"], chunk["dist_x"])
+            sum_ps = ps_denom.tile([P, PACK, P], F32, name="sum_ps", tag="sum_ps")
+            raise_clock(sum_ps[:, 0, :CLOCK_COLS], CLOCK_COLS)
             for j in range(PACK):
-                for i, term in enumerate(terms):
-                    nc.tensor.matmul(
-                        out=denom_ps[:, j, :],
-                        lhsT=term[:, j, cols],
-                        rhs=identity[:],
-                        is_transpose=True,
-                        start=(i == 0),
-                        stop=(i == len(terms) - 1),
-                    )
-            chunk["denom", u] = denom_ps
+                if c in TURNED:
+                    terms = [chunk[name][:, j, cols] for name in ("clipped", "dist_y", "dist_x")]
+                else:
+                    rows = slice(j * P, (j + 1) * P)
+                    terms = [chunk[name][:, u, rows] for name in ("dist_y", "dist_x")]
+                turned_sum(sum_ps[:, j, :], terms)
+            chunk["sum", u] = sum_ps
 
-        def roots(c, u):
+        def add_clipped(c):
             chunk = chunks[c]
-            root = work.tile([P, PACK, P], F32, name="root")
+            denom = work.tile([P, PACK, COLS], F32, name="denom")
+            for u in range(COL_BLOCKS):
+                cols = slice(u * P, (u + 1) * P)
+                nc.vector.tensor_tensor(
+                    out=denom[:, :, cols],
+                    in0=chunk["sum", u][:],
+                    in1=chunk["clipped"][:, :, cols],
+                    op=ALU.add,
+                )
+            chunk["denom"] = denom
+
+        def root(target, source, bias):
             nc.scalar.activation(
-                out=root[:],
-                in_=chunk["denom", u][:],
-                func=FUNC.Abs_reciprocal_sqrt,
-                bias=chunk["bias"][:, u : u + 1],
+                out=target, in_=source, func=FUNC.Abs_reciprocal_sqrt, bias=bias
             )
-            chunk["root", u] = root
 
-        def squares(c, u):
+        def roots(c, half):
             chunk = chunks[c]
-            recip = work.tile([P, PACK, P], F32, name="recip")
-            nc.scalar.activation(out=recip[:], in_=chunk["root", u][:], func=FUNC.Square)
-            chunk["recip", u] = recip
+            if "root" not in chunk:
+                root_tile = work.tile([P, PACK * COLS], F32, name="root_tile")
+                chunk["root"] = root_tile
+            n = PACK * COLS // 2
+            halves = chunk["root"][:].rearrange("p (h n) -> p h n", h=2)
+            if c in TURNED:
+                root(
+                    halves[:, half, :],
+                    chunk["sum", half][:].rearrange("q j p -> q (j p)"),
+                    chunk["bias"][:, half : half + 1],
+                )
+            elif c in Y_ON_SCALAR:
+                denom = chunk["denom"][:].rearrange("p j c -> p (j c)")
+                root(halves[:, half, :], denom[:, half * n : (half + 1) * n], beta[:])
+            else:
+                rows = chunk["root"][:].rearrange("p (j c) -> p j c", j=PACK)
+                for j in range(half * PACK // 2, (half + 1) * PACK // 2):
+                    root(rows[:, j, :], chunk["denom"][:, j, :], chunk["bias"][:, j : j + 1])
+
+        def squares(c, half):
+            chunk = chunks[c]
+            if "recip" not in chunk:
+                recip = work.tile([P, PACK * COLS], F32, name="recip")
+                chunk["recip"] = recip
+            n = PACK * COLS // 2
+            part = slice(half * n, (half + 1) * n)
+            nc.scalar.activation(
+                out=chunk["recip"][:, part], in_=chunk["root"][:, part], func=FUNC.Square
+            )
 
         def turn_back(c, u):
             chunk = chunks[c]
             recip_ps = ps_recip.tile([P, PACK, P], F32, name="recip_ps", tag="recip_ps")
+            recip = chunk["recip"][:].rearrange("q (u j p) -> q u j p", u=COL_BLOCKS, j=PACK)
             for j in range(PACK):
-                nc.tensor.transpose(
-                    out=recip_ps[:, j, :], in_=chunk["recip", u][:, j, :], identity=identity[:]
-                )
+                turned_sum(recip_ps[:, j, :], [recip[:, u, j, :]])
             chunk["recip_ps", u] = recip_ps
+
+        def first_factors(c, half):
+            chunk = chunks[c]
+            if "partial" not in chunk:
+                partial = work.tile([P, PACK, COLS], F32, name="partial")
+                chunk["partial"] = partial
+            js = slice(half * PACK // 2, (half + 1) * PACK // 2)
+            nc.vector.tensor_tensor(
+                out=chunk["partial"][:, js, :],
+                in0=chunk["numer"][:, js, :],
+                in1=chunk["root"][:].rearrange("p (j c) -> p j c", j=PACK)[:, js, :],
+                op=ALU.mult,
+            )
 
         def products(c, u):
             chunk = chunks[c]
             cols = slice(u * P, (u + 1) * P)
+            factor = chunk["numer"]
+            if c in TURNED:
+                recip = chunk["recip_ps", u][:]
+            elif c in VECTOR_SQUARES:
+                factor = chunk["partial"]
+                recip = chunk["root"][:].rearrange("p (j c) -> p j c", j=PACK)[:, :, cols]
+            else:
+                recip = chunk["recip"][:].rearrange("p (j c) -> p j c", j=PACK)[:, :, cols]
             nc.vector.tensor_tensor(
                 out=chunk["grouped"][:, cols, :].rearrange("p (a i) j -> p a j i", i=4),
-                in0=chunk["recip_ps", u][:].rearrange("p j (a i) -> p a j i", i=4),
-                in1=chunk["numer"][:, :, cols].rearrange("p j (a i) -> p a j i", i=4),
+                in0=recip.rearrange("p j (a i) -> p a j i", i=4),
+                in1=factor[:, :, cols].rearrange("p j (a i) -> p a j i", i=4),
                 op=ALU.mult,
             )
 
@@ -292,7 +400,7 @@ def tile_physicalneuralnetwork_s_kernel(
         xT = []
 
         def transpose_x():
-            xT.append(ps_recip.tile([P, PACK, B], BF16, name="xT_ps", tag="recip_ps"))
+            xT.append(psum.tile([P, PACK, B], BF16, name="xT_ps", tag="first_y_then_x"))
             for j in range(PACK):
                 nc.tensor.transpose(
                     out=xT[0][:, j, :], in_=x_sb[:, j * P : (j + 1) * P], identity=identity_bf[:]
@@ -308,89 +416,103 @@ def tile_physicalneuralnetwork_s_kernel(
                 in_=x_grouped[:].rearrange("p b j -> p (b j)"),
             )
 
-        def first_product():
-            tags = ("first_x_then_hid0", "rest_x_then_hid1")
-            for g in range(H_PASSES):
-                hid_ps.append(psum.tile([P, PACK, B], F32, name="hid_ps%d" % g, tag=tags[g]))
-                for t in range(PACK):
-                    unit_cols = slice((g * PACK + t) * P, (g * PACK + t + 1) * P)
-                    nc.tensor.matmul_mx(
-                        out=hid_ps[g][:, t, :],
-                        lhsT=w1_codes[:, unit_cols].bitcast(FP8X4),
-                        lhsT_scale=w1_scales[:, unit_cols],
-                        rhs=x_codes[:].bitcast(FP8X4),
-                        rhs_scale=x_scales[:],
-                        start=True,
-                        stop=True,
-                    )
-
-        def add_b1():
-            nc.vector.tensor_copy(out=b1_col[:], in_=b1_bf[:])
-            for g in range(H_PASSES):
-                nc.vector.tensor_tensor(
-                    out=hid_pre[:, g],
-                    in0=hid_ps[g][:].rearrange("q t b -> q b t"),
-                    in1=b1_col[:, g * PACK : (g + 1) * PACK]
-                    .unsqueeze(1)
-                    .to_broadcast([P, B, PACK]),
-                    op=ALU.add,
+        def first_product(g):
+            hid_ps.append(psum.tile([P, PACK, B], F32, name="hid_ps%d" % g, tag="first_x_then_hid"))
+            for t in range(PACK):
+                unit_cols = slice((g * PACK + t) * P, (g * PACK + t + 1) * P)
+                nc.tensor.matmul_mx(
+                    out=hid_ps[g][:, t, :],
+                    lhsT=w1_codes[:, unit_cols].bitcast(FP8X4),
+                    lhsT_scale=w1_scales[:, unit_cols],
+                    rhs=x_codes[:].bitcast(FP8X4),
+                    rhs_scale=x_scales[:],
+                    start=True,
+                    stop=True,
                 )
 
-        x_distances(0, range(PACK))
-        nc.scalar.activation(out=hid_y[:, COLS:H], in_=rest_y[:], func=FUNC.Copy, scale=2.0 * LS)
-        y_distances(0)
+        def add_b1(g):
+            nc.vector.tensor_tensor(
+                out=hid_pre[:, g],
+                in0=hid_ps[g][:].rearrange("q t b -> q b t"),
+                in1=b1_col[:, g * PACK : (g + 1) * PACK]
+                .unsqueeze(1)
+                .to_broadcast([P, B, PACK]),
+                op=ALU.add,
+            )
+
+        scaled(in_ls[:], in_blk[:], LS)
+        scaled(in_2ls[:], in_blk[:], 2.0 * LS)
         clip_weights(0)
-        column_bias(hid_bias[:], hid_blk[:, :, 1])
+        scaled(hid_2ls_row[:, :COLS], first_y[:], 2.0 * LS)
+        y_distances(0)
+        x_distances(0, 0)
+        x_distances(0, 1)
+        nc.scalar.activation(
+            out=hid_2ls_row[:, COLS : 2 * COLS], in_=second_xy[:, 1, :], func=FUNC.Copy, scale=2.0 * LS
+        )
+        turn(0, 0)
+        turn(0, 1)
+        y_bias(hid_bias[:], hid_blk[:, :, 1])
         numerators(0)
         y_distances(1)
-        x_distances(1, range(PACK))
+        x_distances(1, 0)
+        x_distances(1, 1)
         clip_weights(1)
-        denominators(0, 0)
-        denominators(0, 1)
+        scaled(hid_2ls_row[:, 2 * COLS :], hid_row[:, :, 1], 2.0 * LS)
+        def at_lead(stage, step, lead, *args):
+            for chunk, due in ((step + lead, True), (step + lead + 1, False)):
+                if 0 <= chunk < n_chunks and (chunk in TURNED) == due:
+                    stage(chunk, *args)
+
         for c in range(n_chunks + 1):
-            more = c + 2 < n_chunks
             if c < n_chunks:
                 roots(c, 0)
-                if more:
-                    x_distances(c + 2, (0, 1))
-                squares(c, 0)
+                at_lead(x_distances, c, 2, 0)
+                if c not in VECTOR_SQUARES:
+                    squares(c, 0)
                 roots(c, 1)
-                if more:
-                    x_distances(c + 2, (2, 3))
-                squares(c, 1)
-            if c + 1 < n_chunks:
-                denominators(c + 1, 0)
-                denominators(c + 1, 1)
-            if c < n_chunks:
+                at_lead(x_distances, c, 2, 1)
+                if c not in VECTOR_SQUARES:
+                    squares(c, 1)
+            at_lead(turn, c, 1, 0)
+            at_lead(turn, c, 1, 1)
+            if c in TURNED:
                 turn_back(c, 0)
                 turn_back(c, 1)
             if c == 1:
                 transpose_x()
+            if c in (4, 6):
+                first_product((c - 4) // 2)
+            if c == 0:
+                scaled(hid_ls[:], hid_blk[:], LS)
+                scaled(hid_2ls[:], hid_blk[:], 2.0 * LS)
+                scaled(out_2ls_row[:], out_row[:, :, 1], 2.0 * LS)
+                scaled(out_ls[:], out_blk[:], LS)
+                scaled(out_2ls[:], out_blk[:], 2.0 * LS)
+                y_bias(out_bias[:], out_blk[:, :, 1])
+                scaled(beta[:], one[:], BETA)
+            if c + 1 < n_chunks and c + 1 not in TURNED:
+                add_clipped(c + 1)
+            at_lead(y_distances, c, 2)
             if 0 <= c - 2 < n_chunks - 1:
                 quantise(c - 2)
-                if c - 2 == w1_chunks - 1:
-                    first_product()
-            if 0 <= c - 1 < n_chunks:
-                products(c - 1, 0)
-            if more:
-                y_distances(c + 2)
-            if 0 <= c - 1 < n_chunks:
-                products(c - 1, 1)
-            if more:
+            if c + 2 < n_chunks:
                 clip_weights(c + 2)
             if c + 1 < n_chunks:
                 numerators(c + 1)
-            if c == 1:
-                scaled(hid_ls[:], hid_blk[:], LS)
-                scaled(hid_2ls[:], hid_blk[:], 2.0 * LS)
-                scaled(out_y[:], out_row_xy[:, :, 1], 2.0 * LS)
-                column_bias(out_bias[:], out_blk[:, :, 1])
+            if 0 <= c - 1 < n_chunks:
+                if c - 1 in VECTOR_SQUARES:
+                    first_factors(c - 1, 0)
+                    first_factors(c - 1, 1)
+                products(c - 1, 0)
+                products(c - 1, 1)
             if c == 2:
                 group_x()
             if c == 3:
                 quantise_x()
-            if c - 3 == w1_chunks - 1:
-                add_b1()
+                nc.vector.tensor_copy(out=b1_col[:], in_=b1_bf[:])
+            if c in (5, 7):
+                add_b1((c - 5) // 2)
 
         hid_bf = keep.tile([P, H_PASSES, B * PACK], BF16, align_bytes=64)
         hid_codes = keep.tile([P, H_PASSES, B], U32, align_bytes=64)
@@ -411,7 +533,7 @@ def tile_physicalneuralnetwork_s_kernel(
         out_pre = keep.tile([P, O], F32)
         out_sb = keep.tile([P, O], F32)
         HALF = O // 2
-        halves = [ps_denom.tile([P, HALF], F32, name="out_ps%d" % h, tag="denom_ps") for h in range(2)]
+        halves = [ps_denom.tile([P, HALF], F32, name="out_ps%d" % h, tag="sum_ps") for h in range(2)]
         for half in range(2):
             o_cols = slice(half * HALF, (half + 1) * HALF)
             for g in range(H_PASSES):

@@ -16,19 +16,20 @@ PACK = 4
 K_PASS = P * PACK
 B, I, H, O = 128, 512, 1024, 512
 H_PASSES = H // K_PASS
-COLS = 256
-COL_BLOCKS = COLS // P
-CLOCK_COLS = 32
-TURNED = (0, 1, 2, 3, 4, 5, 6, 7)
-Y_ON_SCALAR = ()
-VECTOR_SQUARES = ()
+COLS = 512
+BLOCKS = COLS // P
+W1_CHUNKS = H // COLS
+CHUNKS = W1_CHUNKS + H_PASSES
+HALF = COLS // 2
 
 RHO_OVER_T = 1.68e-8 / 35e-6
 W_LIMIT = 3.0
 WIDTH_SLOPE = (5.0 - 0.09) / (2.0 * W_LIMIT)
-WIDTH_MID = 0.09 + W_LIMIT * WIDTH_SLOPE
-BETA = WIDTH_MID / WIDTH_SLOPE
+BETA = 0.09 / WIDTH_SLOPE + W_LIMIT
 LS = RHO_OVER_T / WIDTH_SLOPE
+L_SCALE = 2.0**-11
+N_SCALE = L_SCALE / (2.0 * LS)
+TINY = 1e-30
 
 FLOPS = 2 * B * I * H + 2 * B * H * O
 
@@ -39,10 +40,8 @@ def tile_physicalneuralnetwork_s_kernel(
     nc = tc.nc
     with ExitStack() as stack:
         keep = stack.enter_context(tc.tile_pool(name="keep", bufs=1))
-        ahead = stack.enter_context(tc.tile_pool(name="ahead", bufs=5))
-        work = stack.enter_context(tc.tile_pool(name="work", bufs=3))
-        ps_denom = stack.enter_context(tc.psum_pool(name="ps_denom", bufs=3))
-        ps_recip = stack.enter_context(tc.psum_pool(name="ps_recip", bufs=3))
+        dists = stack.enter_context(tc.tile_pool(name="dists", bufs=8))
+        ps_sum = stack.enter_context(tc.psum_pool(name="ps_sum", bufs=4))
         psum = stack.enter_context(tc.psum_pool(name="psum", bufs=1))
         stack.enter_context(tc.manual_schedule())
 
@@ -51,363 +50,246 @@ def tile_physicalneuralnetwork_s_kernel(
         identity_bf = keep.tile([P, P], BF16)
         make_identity(nc, identity_bf[:])
 
-        in_blk = keep.tile([P, PACK, 2], BF16)
-        nc.sync.dma_start(out=in_blk[:], in_=input_positions.rearrange("(j p) c -> p j c", p=P))
+        def load(target, source):
+            nc.sync.dma_start(out=target, in_=source)
+
+        in_blk = keep.tile([P, I // P, 2], BF16)
+        load(in_blk[:], input_positions.rearrange("(j p) c -> p j c", p=P))
         hid_blk = keep.tile([P, H // P, 2], BF16)
-        nc.sync.dma_start(out=hid_blk[:], in_=hidden_positions.rearrange("(m r) c -> r m c", r=P))
+        load(hid_blk[:], hidden_positions.rearrange("(m r) c -> r m c", r=P))
+        w_rows = []
         w1_view = W1.rearrange("(j p) h -> p j h", p=P)
-        w1_sb = []
-        for part in range(H // COLS):
+        for part in range(W1_CHUNKS):
             w1_part = keep.tile([P, PACK, COLS], BF16, name="w1_part%d" % part)
-            nc.sync.dma_start(out=w1_part[:], in_=w1_view[:, :, part * COLS : (part + 1) * COLS])
-            w1_sb.append(w1_part)
-            if part == 1:
-                hid_row = keep.tile([P, H // 2, 2], BF16)
-                nc.sync.dma_start(
-                    out=hid_row[:].rearrange("p h c -> p (h c)"),
-                    in_=hidden_positions[H // 2 :, :]
-                    .rearrange("h c -> (h c)")
-                    .partition_broadcast(P),
-                )
-        x_sb = keep.tile([P, I], BF16)
-        nc.sync.dma_start(out=x_sb[:], in_=x)
-        out_row = keep.tile([P, O, 2], BF16)
-        nc.sync.dma_start(
-            out=out_row[:].rearrange("p o c -> p (o c)"),
-            in_=output_positions.rearrange("o c -> (o c)").partition_broadcast(P),
-        )
+            load(w1_part[:], w1_view[:, :, part * COLS : (part + 1) * COLS])
+            w_rows.append(w1_part)
         out_blk = keep.tile([P, O // P, 2], BF16)
-        nc.sync.dma_start(out=out_blk[:], in_=output_positions.rearrange("(m r) c -> r m c", r=P))
-        w2_sb = keep.tile([P, H_PASSES, PACK, O], BF16)
+        load(out_blk[:], output_positions.rearrange("(m r) c -> r m c", r=P))
         for g in range(H_PASSES):
-            nc.sync.dma_start(
-                out=w2_sb[:, g, :, :],
-                in_=W2[g * K_PASS : (g + 1) * K_PASS, :].rearrange("(j p) o -> p j o", p=P),
-            )
-        b1_bf = keep.tile([P, H // P], BF16)
+            w2_part = keep.tile([P, PACK, O], BF16, name="w2_part%d" % g)
+            load(w2_part[:], W2[g * K_PASS : (g + 1) * K_PASS, :].rearrange("(j p) o -> p j o", p=P))
+            w_rows.append(w2_part)
+        x_sb = keep.tile([P, I], BF16)
+        load(x_sb[:], x)
+        b1_col = keep.tile([P, H // P], BF16)
         with nc.allow_non_contiguous_dma(reason="1,024 bias values, one to a partition and block"):
-            nc.sync.dma_start(out=b1_bf[:], in_=b1.rearrange("(m r) -> r m", r=P))
+            load(b1_col[:], b1.rearrange("(m r) -> r m", r=P))
         b2_row = keep.tile([P, O], BF16)
-        nc.sync.dma_start(out=b2_row[:], in_=b2.partition_broadcast(P))
+        load(b2_row[:], b2.partition_broadcast(P))
 
         one = keep.tile([P, 1], F32)
         nc.vector.memset(one[:], 1.0)
         table_warmer = keep.tile([P, 1], F32)
-        nc.scalar.activation(out=table_warmer[:], in_=one[:], func=FUNC.Abs_reciprocal_sqrt)
+        nc.scalar.activation(out=table_warmer[:], in_=one[:], func=FUNC.Ln)
+        n_bias = keep.tile([P, 1], F32)
+        nc.vector.tensor_scalar(
+            out=n_bias[:], in0=one[:], scalar1=BETA * N_SCALE, scalar2=None, op0=ALU.mult
+        )
+        tiny = keep.tile([P, 1], F32)
+        nc.vector.tensor_scalar(out=tiny[:], in0=one[:], scalar1=TINY, scalar2=None, op0=ALU.mult)
 
         x_codes = keep.tile([P, B], U32, align_bytes=64)
         x_scales = keep.tile([P, B], U8, align_bytes=64)
-        w1_grouped = keep.tile([P, H, PACK], BF16, align_bytes=64)
         w1_codes = keep.tile([P, H], U32, align_bytes=64)
         w1_scales = keep.tile([P, H], U8, align_bytes=64)
-        w2_grouped = keep.tile([P, H_PASSES, O, PACK], BF16, align_bytes=64)
         w2_codes = keep.tile([P, H_PASSES, O], U32, align_bytes=64)
         w2_scales = keep.tile([P, H_PASSES, O], U8, align_bytes=64)
+        hid_codes = keep.tile([P, H_PASSES, B], U32, align_bytes=64)
+        hid_scales = keep.tile([P, H_PASSES, B], U8, align_bytes=64)
 
-        first_x = psum.tile([P, COLS], BF16, name="first_x", tag="first_x_then_hid")
-        first_y = psum.tile([P, COLS], BF16, name="first_y", tag="first_y_then_x")
-        second_xy = ps_recip.tile([P, 2, COLS], BF16, name="second_xy", tag="recip_ps")
+        spreads = {}
+        tables = {}
 
-        def spread(target, chunk, c):
-            for u in range(COL_BLOCKS):
-                m = chunk * COL_BLOCKS + u
+        def spread(name, tag, words, first):
+            bank = psum.tile([P, K_PASS], F32, name="spread_" + name, tag=tag)
+            for i in range(PACK):
                 nc.tensor.transpose(
-                    out=target[:, u * P : (u + 1) * P],
-                    in_=hid_blk[:, m, c : c + 1].to_broadcast([P, P]),
-                    identity=identity_bf[:],
+                    out=bank[:, i * P : (i + 1) * P],
+                    in_=words[:, first + i : first + i + 1].to_broadcast([P, P]),
+                    identity=identity[:],
                 )
+            spreads[name] = bank
 
-        def raise_clock(target, width):
-            nc.tensor.matmul(
-                out=target, lhsT=identity[:], rhs=identity[:, :width], start=True, stop=True
-            )
+        def words_of(blk):
+            return blk[:].rearrange("p n c -> p (n c)").bitcast(F32)
 
-        clock_ps = ps_denom.tile([P, PACK, P], F32, name="clock_ps", tag="sum_ps")
-        for j in range(2):
-            raise_clock(clock_ps[:, j, :], P)
-        spread(first_x[:], 0, 0)
-        spread(first_y[:], 0, 1)
-        spread(second_xy[:, 1, :], 1, 1)
-        spread(second_xy[:, 0, :], 1, 0)
-        w1_chunks = H // COLS
+        def keep_table(name):
+            table = keep.tile([P, K_PASS], F32, name="table_" + name)
+            nc.scalar.copy(out=table[:], in_=spreads[name][:])
+            tables[name] = table
 
-        in_ls = keep.tile([P, PACK, 2], F32)
-        in_2ls = keep.tile([P, PACK, 2], F32)
-        hid_ls = keep.tile([P, H // P, 2], F32)
-        hid_2ls = keep.tile([P, H // P, 2], F32)
-        hid_bias = keep.tile([P, H // P], F32)
-        out_ls = keep.tile([P, O // P, 2], F32)
-        out_2ls = keep.tile([P, O // P, 2], F32)
-        out_bias = keep.tile([P, O // P], F32)
-        beta = keep.tile([P, 1], F32)
+        def pairs(name):
+            return tables[name][:].bitcast(BF16).rearrange("p (n c) -> p n c", c=2)
 
-        def scaled(target, source, factor):
+        hid_half = keep.tile([P, H // P, 2], BF16)
+        out_half = keep.tile([P, O // P, 2], BF16)
+        in_scaled = keep.tile([P, I // P, 2], F32)
+        hid_scaled = keep.tile([P, H // P, 2], F32)
+        in_rest = keep.tile([P, I // P], F32)
+        hid_rest = keep.tile([P, H // P], F32)
+
+        def times(target, source, factor):
             nc.vector.tensor_scalar(
                 out=target, in0=source, scalar1=factor, scalar2=None, op0=ALU.mult
             )
 
-        def y_bias(target, source):
-            nc.vector.tensor_scalar(
-                out=target, in0=source, scalar1=-LS, scalar2=BETA, op0=ALU.mult, op1=ALU.add
+        def row_rests(rest, scaled, blk):
+            times(scaled[:], blk[:], -0.5)
+            nc.vector.tensor_tensor(
+                out=rest[:], in0=scaled[:, :, 0], in1=scaled[:, :, 1], op=ALU.add
             )
-
-        hid_2ls_row = keep.tile([P, H], F32)
-        out_2ls_row = keep.tile([P, O], F32)
 
         chunks = []
-        for part in range(w1_chunks):
+        for part in range(W1_CHUNKS):
             cols = slice(part * COLS, (part + 1) * COLS)
-            blocks = slice(part * COL_BLOCKS, (part + 1) * COL_BLOCKS)
-            chunk = {
-                "w_rows": w1_sb[part][:],
-                "grouped": w1_grouped[:, cols, :],
-                "codes": w1_codes[:, cols],
-                "scales": w1_scales[:, cols],
-            }
-            if part == 0:
-                chunk["free_x"] = first_x[:]
-            elif part == 1:
-                chunk["free_x"] = second_xy[:, 0, :]
-            else:
-                chunk["free_x"] = hid_row[:, (part - 2) * COLS : (part - 1) * COLS, 0]
-            chunk["free_2ls_y"] = hid_2ls_row[:, cols]
-            chunk["part_ls"] = in_ls[:]
-            chunk["part_2ls"] = in_2ls[:]
-            chunk["bias"] = hid_bias[:, blocks]
-            chunks.append(chunk)
-        for g in range(H_PASSES):
-            for part in range(O // COLS):
-                cols = slice(part * COLS, (part + 1) * COLS)
-                blocks = slice(part * COL_BLOCKS, (part + 1) * COL_BLOCKS)
-                k_blocks = slice(g * PACK, (g + 1) * PACK)
-                k_rows = slice(g * K_PASS, (g + 1) * K_PASS)
-                chunk = {
-                    "w_rows": w2_sb[:, g, :, cols],
-                    "grouped": w2_grouped[:, g, cols, :],
-                    "codes": w2_codes[:, g, cols],
-                    "scales": w2_scales[:, g, cols],
+            chunks.append(
+                {
+                    "table": "in",
+                    "col_blk": hid_blk,
+                    "col_half": hid_half,
+                    "m": part * BLOCKS,
+                    "rest": "in_rest",
+                    "codes": w1_codes[:, cols],
+                    "scales": w1_scales[:, cols],
                 }
-                if len(chunks) in TURNED:
-                    chunk["free_x"] = out_row[:, cols, 0]
-                    chunk["free_2ls_y"] = out_2ls_row[:, cols]
-                    chunk["part_ls"] = hid_ls[:, k_blocks, :]
-                    chunk["part_2ls"] = hid_2ls[:, k_blocks, :]
-                    chunk["bias"] = out_bias[:, blocks]
-                else:
-                    chunk["free_x"] = hid_row[:, :, 0]
-                    chunk["free_y"] = hid_row[:, :, 1]
-                    chunk["free_2ls_y"] = hid_2ls_row[:, k_rows]
-                    chunk["part_ls"] = out_ls[:, blocks, :]
-                    chunk["part_2ls"] = out_2ls[:, blocks, :]
-                    chunk["bias"] = hid_bias[:, k_blocks]
-                chunks.append(chunk)
-        n_chunks = len(chunks)
-
-        def abs_distances(c, i, coordinate, free, target):
-            nc.scalar.activation(
-                out=target,
-                in_=free,
-                func=FUNC.Abs,
-                scale=-LS,
-                bias=chunks[c]["part_ls"][:, i, coordinate : coordinate + 1],
             )
+        for g in range(H_PASSES):
+            chunks.append(
+                {
+                    "table": "hid%d" % g,
+                    "col_blk": out_blk,
+                    "col_half": out_half,
+                    "m": 0,
+                    "rest": "hid%d_rest" % g,
+                    "codes": w2_codes[:, g, :],
+                    "scales": w2_scales[:, g, :],
+                }
+            )
+        for c, chunk in enumerate(chunks):
+            chunk["rows"] = w_rows[c]
+            for name, dtype in (("clipped", BF16), ("log_n", F32), ("log_l", F32), ("diff", F32)):
+                made = keep.tile([P, PACK, COLS], dtype, name="%s%d" % (name, c))
+                chunk[name] = made
+            grouped = keep.tile([P, COLS, PACK], BF16, name="grouped%d" % c, align_bytes=64)
+            chunk["grouped"] = grouped
 
-        def distance_tile(c, name):
+        def distances(c, u):
             chunk = chunks[c]
-            if name not in chunk:
-                blocks = PACK if c in TURNED else COL_BLOCKS
-                tile = work.tile([P, blocks, PACK * COLS // blocks], F32, name=name)
-                chunk[name] = tile
-            return chunk[name]
-
-        def x_distances(c, half):
-            dist_x = distance_tile(c, "dist_x")
-            n = (PACK if c in TURNED else COL_BLOCKS) // 2
-            for i in range(half * n, (half + 1) * n):
-                abs_distances(c, i, 0, chunks[c]["free_x"], dist_x[:, i, :])
-                if c in Y_ON_SCALAR:
-                    dist_y = distance_tile(c, "dist_y")
-                    abs_distances(c, i, 1, chunks[c]["free_y"], dist_y[:, i, :])
-
-        def y_distances(c):
-            if c in Y_ON_SCALAR:
-                return
-            chunk = chunks[c]
-            dist_y = distance_tile(c, "dist_y")
-            for i in range(PACK if c in TURNED else COL_BLOCKS):
+            m = chunk["m"] + u
+            dist = dists.tile([P, 2, K_PASS], F32, name="dist")
+            for xy in range(2):
                 nc.vector.tensor_scalar(
-                    out=dist_y[:, i, :],
-                    in0=chunk["free_2ls_y"],
-                    scalar1=chunk["part_2ls"][:, i, 1:2],
-                    scalar2=chunk["part_ls"][:, i, 1:2],
+                    out=dist[:, xy, :],
+                    in0=pairs(chunk["table"])[:, :, xy],
+                    scalar1=chunk["col_blk"][:, m, xy : xy + 1],
+                    scalar2=chunk["col_half"][:, m, xy : xy + 1],
                     op0=ALU.max,
                     op1=ALU.subtract,
                 )
+            chunk["dist", u] = dist
+
+        def turn(c, js):
+            chunk = chunks[c]
+            for j in js:
+                length = ps_sum.tile([P, COLS], F32, name="length")
+                chunk["length", j] = length
+            for u in range(BLOCKS):
+                for j in js:
+                    k_cols = slice(j * P, (j + 1) * P)
+                    terms = (
+                        chunk["dist", u][:, 0, k_cols],
+                        chunk["dist", u][:, 1, k_cols],
+                        tables[chunk["rest"]][:, k_cols],
+                    )
+                    for i, term in enumerate(terms):
+                        nc.tensor.matmul(
+                            out=chunk["length", j][:, u * P : (u + 1) * P],
+                            lhsT=term,
+                            rhs=identity[:],
+                            is_transpose=True,
+                            start=(i == 0),
+                            stop=(i == len(terms) - 1),
+                        )
+
+        def log_lengths(c, js):
+            for j in js:
+                nc.scalar.activation(
+                    out=chunks[c]["log_l"][:, j, :],
+                    in_=chunks[c]["length", j][:],
+                    func=FUNC.Ln,
+                    scale=L_SCALE,
+                    bias=tiny[:],
+                )
 
         def clip_weights(c):
-            chunk = chunks[c]
-            dtype, name = (F32, "clipped") if c in TURNED else (BF16, "clipped_bf")
-            clipped = ahead.tile([P, PACK, COLS], dtype, name=name)
             nc.vector.tensor_scalar(
-                out=clipped[:],
-                in0=chunk["w_rows"],
+                out=chunks[c]["clipped"][:],
+                in0=chunks[c]["rows"][:],
                 scalar1=-W_LIMIT,
                 scalar2=W_LIMIT,
                 op0=ALU.max,
                 op1=ALU.min,
             )
-            chunk["clipped"] = clipped
 
-        def numerators(c):
-            chunk = chunks[c]
-            numer = ahead.tile([P, PACK, COLS], F32, name="numer")
-            nc.vector.scalar_tensor_tensor(
-                out=numer[:],
-                in0=chunk["clipped"][:],
-                scalar=BETA,
-                in1=chunk["w_rows"],
-                op0=ALU.add,
-                op1=ALU.mult,
-            )
-            chunk["numer"] = numer
-
-        def turned_sum(target, terms):
-            for i, term in enumerate(terms):
-                nc.tensor.matmul(
-                    out=target,
-                    lhsT=term,
-                    rhs=identity[:],
-                    is_transpose=True,
-                    start=(i == 0),
-                    stop=(i == len(terms) - 1),
-                )
-
-        def turn(c, u):
-            chunk = chunks[c]
-            cols = slice(u * P, (u + 1) * P)
-            sum_ps = ps_denom.tile([P, PACK, P], F32, name="sum_ps", tag="sum_ps")
-            raise_clock(sum_ps[:, 0, :CLOCK_COLS], CLOCK_COLS)
-            for j in range(PACK):
-                if c in TURNED:
-                    terms = [chunk[name][:, j, cols] for name in ("clipped", "dist_y", "dist_x")]
-                else:
-                    rows = slice(j * P, (j + 1) * P)
-                    terms = [chunk[name][:, u, rows] for name in ("dist_y", "dist_x")]
-                turned_sum(sum_ps[:, j, :], terms)
-            chunk["sum", u] = sum_ps
-
-        def add_clipped(c):
-            chunk = chunks[c]
-            denom = work.tile([P, PACK, COLS], F32, name="denom")
-            for u in range(COL_BLOCKS):
-                cols = slice(u * P, (u + 1) * P)
-                nc.vector.tensor_tensor(
-                    out=denom[:, :, cols],
-                    in0=chunk["sum", u][:],
-                    in1=chunk["clipped"][:, :, cols],
-                    op=ALU.add,
-                )
-            chunk["denom"] = denom
-
-        def root(target, source, bias):
+        def log_widths(c):
             nc.scalar.activation(
-                out=target, in_=source, func=FUNC.Abs_reciprocal_sqrt, bias=bias
+                out=chunks[c]["log_n"][:],
+                in_=chunks[c]["clipped"][:],
+                func=FUNC.Ln,
+                scale=N_SCALE,
+                bias=n_bias[:],
             )
 
-        def roots(c, half):
-            chunk = chunks[c]
-            if "root" not in chunk:
-                root_tile = work.tile([P, PACK * COLS], F32, name="root_tile")
-                chunk["root"] = root_tile
-            n = PACK * COLS // 2
-            halves = chunk["root"][:].rearrange("p (h n) -> p h n", h=2)
-            if c in TURNED:
-                root(
-                    halves[:, half, :],
-                    chunk["sum", half][:].rearrange("q j p -> q (j p)"),
-                    chunk["bias"][:, half : half + 1],
-                )
-            elif c in Y_ON_SCALAR:
-                denom = chunk["denom"][:].rearrange("p j c -> p (j c)")
-                root(halves[:, half, :], denom[:, half * n : (half + 1) * n], beta[:])
-            else:
-                rows = chunk["root"][:].rearrange("p (j c) -> p j c", j=PACK)
-                for j in range(half * PACK // 2, (half + 1) * PACK // 2):
-                    root(rows[:, j, :], chunk["denom"][:, j, :], chunk["bias"][:, j : j + 1])
-
-        def squares(c, half):
-            chunk = chunks[c]
-            if "recip" not in chunk:
-                recip = work.tile([P, PACK * COLS], F32, name="recip")
-                chunk["recip"] = recip
-            n = PACK * COLS // 2
-            part = slice(half * n, (half + 1) * n)
-            nc.scalar.activation(
-                out=chunk["recip"][:, part], in_=chunk["root"][:, part], func=FUNC.Square
-            )
-
-        def turn_back(c, u):
-            chunk = chunks[c]
-            recip_ps = ps_recip.tile([P, PACK, P], F32, name="recip_ps", tag="recip_ps")
-            recip = chunk["recip"][:].rearrange("q (u j p) -> q u j p", u=COL_BLOCKS, j=PACK)
-            for j in range(PACK):
-                turned_sum(recip_ps[:, j, :], [recip[:, u, j, :]])
-            chunk["recip_ps", u] = recip_ps
-
-        def first_factors(c, half):
-            chunk = chunks[c]
-            if "partial" not in chunk:
-                partial = work.tile([P, PACK, COLS], F32, name="partial")
-                chunk["partial"] = partial
-            js = slice(half * PACK // 2, (half + 1) * PACK // 2)
+        def differences(c, js):
+            rows = slice(js[0], js[-1] + 1)
             nc.vector.tensor_tensor(
-                out=chunk["partial"][:, js, :],
-                in0=chunk["numer"][:, js, :],
-                in1=chunk["root"][:].rearrange("p (j c) -> p j c", j=PACK)[:, js, :],
-                op=ALU.mult,
+                out=chunks[c]["diff"][:, rows, :],
+                in0=chunks[c]["log_n"][:, rows, :],
+                in1=chunks[c]["log_l"][:, rows, :],
+                op=ALU.subtract,
             )
 
-        def products(c, u):
+        def factors(c, half):
+            cols = slice(half * HALF, (half + 1) * HALF)
+            nc.scalar.activation(
+                out=chunks[c]["log_l"][:, :, cols],
+                in_=chunks[c]["diff"][:, :, cols],
+                func=FUNC.Sigmoid,
+            )
+
+        def products(c, half):
             chunk = chunks[c]
-            cols = slice(u * P, (u + 1) * P)
-            factor = chunk["numer"]
-            if c in TURNED:
-                recip = chunk["recip_ps", u][:]
-            elif c in VECTOR_SQUARES:
-                factor = chunk["partial"]
-                recip = chunk["root"][:].rearrange("p (j c) -> p j c", j=PACK)[:, :, cols]
-            else:
-                recip = chunk["recip"][:].rearrange("p (j c) -> p j c", j=PACK)[:, :, cols]
+            cols = slice(half * HALF, (half + 1) * HALF)
             nc.vector.tensor_tensor(
                 out=chunk["grouped"][:, cols, :].rearrange("p (a i) j -> p a j i", i=4),
-                in0=recip.rearrange("p j (a i) -> p a j i", i=4),
-                in1=factor[:, :, cols].rearrange("p j (a i) -> p a j i", i=4),
+                in0=chunk["log_l"][:, :, cols].rearrange("p j (a i) -> p a j i", i=4),
+                in1=chunk["rows"][:, :, cols].rearrange("p j (a i) -> p a j i", i=4),
                 op=ALU.mult,
             )
 
-        def quantise(c):
-            chunk = chunks[c]
+        def quantise(c, half):
+            cols = slice(half * HALF, (half + 1) * HALF)
             nc.vector.quantize_mx(
-                out=chunk["codes"].bitcast(FP8X4),
-                scales=chunk["scales"],
-                in_=chunk["grouped"].rearrange("p c j -> p (c j)"),
+                out=chunks[c]["codes"][:, cols].bitcast(FP8X4),
+                scales=chunks[c]["scales"][:, cols],
+                in_=chunks[c]["grouped"][:, cols, :].rearrange("p c j -> p (c j)"),
             )
 
         x_grouped = keep.tile([P, B, PACK], BF16, align_bytes=64)
-        b1_col = keep.tile([P, H // P], F32)
         hid_pre = keep.tile([P, H_PASSES, B, PACK], F32)
-        hid_ps = []
-        xT = []
+        hid_bf = keep.tile([P, H_PASSES, B * PACK], BF16, align_bytes=64)
+        banks = {}
 
         def transpose_x():
-            xT.append(psum.tile([P, PACK, B], BF16, name="xT_ps", tag="first_y_then_x"))
+            xT = psum.tile([P, PACK, B], BF16, name="xT", tag="hid0_then_x")
             for j in range(PACK):
                 nc.tensor.transpose(
-                    out=xT[0][:, j, :], in_=x_sb[:, j * P : (j + 1) * P], identity=identity_bf[:]
+                    out=xT[:, j, :], in_=x_sb[:, j * P : (j + 1) * P], identity=identity_bf[:]
                 )
+            banks["xT"] = xT
 
         def group_x():
-            nc.scalar.copy(out=x_grouped[:], in_=xT[0][:].rearrange("p j b -> p b j"))
+            nc.vector.tensor_copy(out=x_grouped[:], in_=banks["xT"][:].rearrange("p j b -> p b j"))
 
         def quantise_x():
             nc.vector.quantize_mx(
@@ -417,11 +299,11 @@ def tile_physicalneuralnetwork_s_kernel(
             )
 
         def first_product(g):
-            hid_ps.append(psum.tile([P, PACK, B], F32, name="hid_ps%d" % g, tag="first_x_then_hid"))
+            hid_ps = psum.tile([P, PACK, B], F32, name="hid_ps%d" % g, tag="in_then_hid")
             for t in range(PACK):
                 unit_cols = slice((g * PACK + t) * P, (g * PACK + t + 1) * P)
                 nc.tensor.matmul_mx(
-                    out=hid_ps[g][:, t, :],
+                    out=hid_ps[:, t, :],
                     lhsT=w1_codes[:, unit_cols].bitcast(FP8X4),
                     lhsT_scale=w1_scales[:, unit_cols],
                     rhs=x_codes[:].bitcast(FP8X4),
@@ -429,127 +311,147 @@ def tile_physicalneuralnetwork_s_kernel(
                     start=True,
                     stop=True,
                 )
+            banks["hid", g] = hid_ps
 
         def add_b1(g):
+            bias = b1_col[:, g * PACK : (g + 1) * PACK].unsqueeze(1).to_broadcast([P, B, PACK])
             nc.vector.tensor_tensor(
                 out=hid_pre[:, g],
-                in0=hid_ps[g][:].rearrange("q t b -> q b t"),
-                in1=b1_col[:, g * PACK : (g + 1) * PACK]
-                .unsqueeze(1)
-                .to_broadcast([P, B, PACK]),
+                in0=banks["hid", g][:].rearrange("q t b -> q b t"),
+                in1=bias,
                 op=ALU.add,
             )
 
-        scaled(in_ls[:], in_blk[:], LS)
-        scaled(in_2ls[:], in_blk[:], 2.0 * LS)
-        clip_weights(0)
-        scaled(hid_2ls_row[:, :COLS], first_y[:], 2.0 * LS)
-        y_distances(0)
-        x_distances(0, 0)
-        x_distances(0, 1)
-        nc.scalar.activation(
-            out=hid_2ls_row[:, COLS : 2 * COLS], in_=second_xy[:, 1, :], func=FUNC.Copy, scale=2.0 * LS
-        )
-        turn(0, 0)
-        turn(0, 1)
-        y_bias(hid_bias[:], hid_blk[:, :, 1])
-        numerators(0)
-        y_distances(1)
-        x_distances(1, 0)
-        x_distances(1, 1)
-        clip_weights(1)
-        scaled(hid_2ls_row[:, 2 * COLS :], hid_row[:, :, 1], 2.0 * LS)
-        def at_lead(stage, step, lead, *args):
-            for chunk, due in ((step + lead, True), (step + lead + 1, False)):
-                if 0 <= chunk < n_chunks and (chunk in TURNED) == due:
-                    stage(chunk, *args)
-
-        for c in range(n_chunks + 1):
-            if c < n_chunks:
-                roots(c, 0)
-                at_lead(x_distances, c, 2, 0)
-                if c not in VECTOR_SQUARES:
-                    squares(c, 0)
-                roots(c, 1)
-                at_lead(x_distances, c, 2, 1)
-                if c not in VECTOR_SQUARES:
-                    squares(c, 1)
-            at_lead(turn, c, 1, 0)
-            at_lead(turn, c, 1, 1)
-            if c in TURNED:
-                turn_back(c, 0)
-                turn_back(c, 1)
-            if c == 1:
-                transpose_x()
-            if c in (4, 6):
-                first_product((c - 4) // 2)
-            if c == 0:
-                scaled(hid_ls[:], hid_blk[:], LS)
-                scaled(hid_2ls[:], hid_blk[:], 2.0 * LS)
-                scaled(out_2ls_row[:], out_row[:, :, 1], 2.0 * LS)
-                scaled(out_ls[:], out_blk[:], LS)
-                scaled(out_2ls[:], out_blk[:], 2.0 * LS)
-                y_bias(out_bias[:], out_blk[:, :, 1])
-                scaled(beta[:], one[:], BETA)
-            if c + 1 < n_chunks and c + 1 not in TURNED:
-                add_clipped(c + 1)
-            at_lead(y_distances, c, 2)
-            if 0 <= c - 2 < n_chunks - 1:
-                quantise(c - 2)
-            if c + 2 < n_chunks:
-                clip_weights(c + 2)
-            if c + 1 < n_chunks:
-                numerators(c + 1)
-            if 0 <= c - 1 < n_chunks:
-                if c - 1 in VECTOR_SQUARES:
-                    first_factors(c - 1, 0)
-                    first_factors(c - 1, 1)
-                products(c - 1, 0)
-                products(c - 1, 1)
-            if c == 2:
-                group_x()
-            if c == 3:
-                quantise_x()
-                nc.vector.tensor_copy(out=b1_col[:], in_=b1_bf[:])
-            if c in (5, 7):
-                add_b1((c - 5) // 2)
-
-        hid_bf = keep.tile([P, H_PASSES, B * PACK], BF16, align_bytes=64)
-        hid_codes = keep.tile([P, H_PASSES, B], U32, align_bytes=64)
-        hid_scales = keep.tile([P, H_PASSES, B], U8, align_bytes=64)
-        for g in range(H_PASSES):
+        def hidden_sigmoid(g):
             nc.scalar.activation(
                 out=hid_bf[:, g, :],
                 in_=hid_pre[:, g].rearrange("q b t -> q (b t)"),
                 func=FUNC.Sigmoid,
             )
-        for g in range(H_PASSES):
+
+        def quantise_hidden(g):
             nc.vector.quantize_mx(
                 out=hid_codes[:, g, :].bitcast(FP8X4), scales=hid_scales[:, g, :], in_=hid_bf[:, g, :]
             )
 
-        quantise(n_chunks - 1)
-
         out_pre = keep.tile([P, O], F32)
         out_sb = keep.tile([P, O], F32)
-        HALF = O // 2
-        halves = [ps_denom.tile([P, HALF], F32, name="out_ps%d" % h, tag="sum_ps") for h in range(2)]
-        for half in range(2):
-            o_cols = slice(half * HALF, (half + 1) * HALF)
+        half_cols = [slice(half * HALF, (half + 1) * HALF) for half in range(2)]
+        out_tags = ("hid1_then_out", "rest_then_out")
+
+        def second_product(half):
+            out_ps = psum.tile([P, HALF], F32, name="out_ps%d" % half, tag=out_tags[half])
             for g in range(H_PASSES):
                 nc.tensor.matmul_mx(
-                    out=halves[half][:],
+                    out=out_ps[:],
                     lhsT=hid_codes[:, g, :].bitcast(FP8X4),
                     lhsT_scale=hid_scales[:, g, :],
-                    rhs=w2_codes[:, g, o_cols].bitcast(FP8X4),
-                    rhs_scale=w2_scales[:, g, o_cols],
+                    rhs=w2_codes[:, g, half_cols[half]].bitcast(FP8X4),
+                    rhs_scale=w2_scales[:, g, half_cols[half]],
                     start=(g == 0),
                     stop=(g == H_PASSES - 1),
                 )
-        for half in range(2):
-            o_cols = slice(half * HALF, (half + 1) * HALF)
+            banks["out", half] = out_ps
+
+        def finish(half):
+            o_cols = half_cols[half]
             nc.vector.tensor_tensor(
-                out=out_pre[:, o_cols], in0=halves[half][:], in1=b2_row[:, o_cols], op=ALU.add
+                out=out_pre[:, o_cols], in0=banks["out", half][:], in1=b2_row[:, o_cols], op=ALU.add
             )
             nc.scalar.activation(out=out_sb[:, o_cols], in_=out_pre[:, o_cols], func=FUNC.Sigmoid)
             nc.sync.dma_start(out=out[:, o_cols], in_=out_sb[:, o_cols])
+
+        low, high = (0, 1), (2, 3)
+        spread("in", "in_then_hid", words_of(in_blk), 0)
+        keep_table("in")
+        row_rests(in_rest, in_scaled, in_blk)
+        spread("in_rest", "rest_then_out", in_rest, 0)
+        times(hid_half[:], hid_blk[:], 0.5)
+        distances(0, 0)
+        distances(0, 1)
+        keep_table("in_rest")
+        clip_weights(0)
+        log_widths(0)
+        distances(0, 2)
+        distances(0, 3)
+        turn(0, low)
+        turn(0, high)
+        log_lengths(0, low)
+        log_lengths(0, high)
+        row_rests(hid_rest, hid_scaled, hid_blk)
+        spread("hid0", "hid0_then_x", words_of(hid_blk), 0)
+        spread("hid1", "hid1_then_out", words_of(hid_blk), PACK)
+        spread("hid0_rest", "rest_then_out", hid_rest, 0)
+        clip_weights(1)
+        for u in range(BLOCKS):
+            distances(1, u)
+        turn(1, low)
+        turn(1, high)
+        keep_table("hid0")
+        keep_table("hid0_rest")
+        log_widths(1)
+        times(out_half[:], out_blk[:], 0.5)
+        differences(0, low)
+        log_lengths(1, low)
+        log_lengths(1, high)
+        keep_table("hid1")
+        spread("hid1_rest", "rest_then_out", hid_rest, PACK)
+        keep_table("hid1_rest")
+        clip_weights(2)
+        log_widths(2)
+        for u in range(BLOCKS):
+            distances(2, u)
+        turn(2, low)
+        turn(2, high)
+        differences(0, high)
+        log_lengths(2, low)
+        log_lengths(2, high)
+        clip_weights(3)
+        log_widths(3)
+        for u in range(BLOCKS):
+            distances(3, u)
+        turn(3, low)
+        turn(3, high)
+        transpose_x()
+        differences(1, low)
+        differences(1, high)
+        differences(2, low)
+        differences(2, high)
+        log_lengths(3, low)
+        log_lengths(3, high)
+        differences(3, low)
+        group_x()
+        differences(3, high)
+        quantise_x()
+
+        parts = [(c, half) for c in range(CHUNKS) for half in range(2)]
+        for part in parts:
+            factors(*part)
+        products(*parts[0])
+        products(*parts[1])
+        quantise(*parts[0])
+        products(*parts[2])
+        quantise(*parts[1])
+        first_product(0)
+        products(*parts[3])
+        quantise(*parts[2])
+        products(*parts[4])
+        quantise(*parts[3])
+        first_product(1)
+        add_b1(0)
+        hidden_sigmoid(0)
+        products(*parts[5])
+        quantise(*parts[4])
+        add_b1(1)
+        hidden_sigmoid(1)
+        products(*parts[6])
+        quantise(*parts[5])
+        quantise_hidden(0)
+        products(*parts[7])
+        quantise(*parts[6])
+        quantise_hidden(1)
+        second_product(0)
+        quantise(*parts[7])
+        second_product(1)
+        finish(0)
+        finish(1)

from contextlib import ExitStack

import concourse.mybir as mybir
from concourse.masks import make_identity

F32 = mybir.dt.float32
BF16 = mybir.dt.bfloat16
U32 = mybir.dt.uint32
U8 = mybir.dt.uint8
FP8X4 = mybir.dt.float8_e4m3fn_x4
ALU = mybir.AluOpType
FUNC = mybir.ActivationFunctionType

P = 128
PACK = 4
K_PASS = P * PACK
B, I, H, O = 128, 512, 1024, 512
H_PASSES = H // K_PASS
COLS = 512
BLOCKS = COLS // P
W1_CHUNKS = H // COLS
CHUNKS = W1_CHUNKS + H_PASSES
HALF = COLS // 2

RHO_OVER_T = 1.68e-8 / 35e-6
W_LIMIT = 3.0
WIDTH_SLOPE = (5.0 - 0.09) / (2.0 * W_LIMIT)
BETA = 0.09 / WIDTH_SLOPE + W_LIMIT
LS = RHO_OVER_T / WIDTH_SLOPE
L_SCALE = 2.0**-11
N_SCALE = L_SCALE / (2.0 * LS)
TINY = 1e-30

FLOPS = 2 * B * I * H + 2 * B * H * O


def tile_physicalneuralnetwork_s_kernel(
    tc, x, W1, b1, W2, b2, input_positions, hidden_positions, output_positions, out
):
    nc = tc.nc
    with ExitStack() as stack:
        keep = stack.enter_context(tc.tile_pool(name="keep", bufs=1))
        dists = stack.enter_context(tc.tile_pool(name="dists", bufs=8))
        ps_sum = stack.enter_context(tc.psum_pool(name="ps_sum", bufs=4))
        psum = stack.enter_context(tc.psum_pool(name="psum", bufs=1))
        stack.enter_context(tc.manual_schedule())

        identity = keep.tile([P, P], F32)
        make_identity(nc, identity[:])
        identity_bf = keep.tile([P, P], BF16)
        make_identity(nc, identity_bf[:])

        def load(target, source):
            nc.sync.dma_start(out=target, in_=source)

        in_blk = keep.tile([P, I // P, 2], BF16)
        load(in_blk[:], input_positions.rearrange("(j p) c -> p j c", p=P))
        hid_blk = keep.tile([P, H // P, 2], BF16)
        load(hid_blk[:], hidden_positions.rearrange("(m r) c -> r m c", r=P))
        w_rows = []
        w1_view = W1.rearrange("(j p) h -> p j h", p=P)
        for part in range(W1_CHUNKS):
            w1_part = keep.tile([P, PACK, COLS], BF16, name="w1_part%d" % part)
            load(w1_part[:], w1_view[:, :, part * COLS : (part + 1) * COLS])
            w_rows.append(w1_part)
        out_blk = keep.tile([P, O // P, 2], BF16)
        load(out_blk[:], output_positions.rearrange("(m r) c -> r m c", r=P))
        for g in range(H_PASSES):
            w2_part = keep.tile([P, PACK, O], BF16, name="w2_part%d" % g)
            load(w2_part[:], W2[g * K_PASS : (g + 1) * K_PASS, :].rearrange("(j p) o -> p j o", p=P))
            w_rows.append(w2_part)
        x_sb = keep.tile([P, I], BF16)
        load(x_sb[:], x)
        b1_col = keep.tile([P, H // P], BF16)
        with nc.allow_non_contiguous_dma(reason="1,024 bias values, one to a partition and block"):
            load(b1_col[:], b1.rearrange("(m r) -> r m", r=P))
        b2_row = keep.tile([P, O], BF16)
        load(b2_row[:], b2.partition_broadcast(P))

        one = keep.tile([P, 1], F32)
        nc.vector.memset(one[:], 1.0)
        table_warmer = keep.tile([P, 1], F32)
        nc.scalar.activation(out=table_warmer[:], in_=one[:], func=FUNC.Ln)
        n_bias = keep.tile([P, 1], F32)
        nc.vector.tensor_scalar(
            out=n_bias[:], in0=one[:], scalar1=BETA * N_SCALE, scalar2=None, op0=ALU.mult
        )
        tiny = keep.tile([P, 1], F32)
        nc.vector.tensor_scalar(out=tiny[:], in0=one[:], scalar1=TINY, scalar2=None, op0=ALU.mult)

        x_codes = keep.tile([P, B], U32, align_bytes=64)
        x_scales = keep.tile([P, B], U8, align_bytes=64)
        w1_codes = keep.tile([P, H], U32, align_bytes=64)
        w1_scales = keep.tile([P, H], U8, align_bytes=64)
        w2_codes = keep.tile([P, H_PASSES, O], U32, align_bytes=64)
        w2_scales = keep.tile([P, H_PASSES, O], U8, align_bytes=64)
        hid_codes = keep.tile([P, H_PASSES, B], U32, align_bytes=64)
        hid_scales = keep.tile([P, H_PASSES, B], U8, align_bytes=64)

        spreads = {}
        tables = {}

        def spread(name, tag, words, first):
            bank = psum.tile([P, K_PASS], F32, name="spread_" + name, tag=tag)
            for i in range(PACK):
                nc.tensor.transpose(
                    out=bank[:, i * P : (i + 1) * P],
                    in_=words[:, first + i : first + i + 1].to_broadcast([P, P]),
                    identity=identity[:],
                )
            spreads[name] = bank

        def words_of(blk):
            return blk[:].rearrange("p n c -> p (n c)").bitcast(F32)

        def keep_table(name):
            table = keep.tile([P, K_PASS], F32, name="table_" + name)
            nc.scalar.copy(out=table[:], in_=spreads[name][:])
            tables[name] = table

        def pairs(name):
            return tables[name][:].bitcast(BF16).rearrange("p (n c) -> p n c", c=2)

        hid_half = keep.tile([P, H // P, 2], BF16)
        out_half = keep.tile([P, O // P, 2], BF16)
        in_scaled = keep.tile([P, I // P, 2], F32)
        hid_scaled = keep.tile([P, H // P, 2], F32)
        in_rest = keep.tile([P, I // P], F32)
        hid_rest = keep.tile([P, H // P], F32)

        def times(target, source, factor):
            nc.vector.tensor_scalar(
                out=target, in0=source, scalar1=factor, scalar2=None, op0=ALU.mult
            )

        def row_rests(rest, scaled, blk):
            times(scaled[:], blk[:], -0.5)
            nc.vector.tensor_tensor(
                out=rest[:], in0=scaled[:, :, 0], in1=scaled[:, :, 1], op=ALU.add
            )

        chunks = []
        for part in range(W1_CHUNKS):
            cols = slice(part * COLS, (part + 1) * COLS)
            chunks.append(
                {
                    "table": "in",
                    "col_blk": hid_blk,
                    "col_half": hid_half,
                    "m": part * BLOCKS,
                    "rest": "in_rest",
                    "codes": w1_codes[:, cols],
                    "scales": w1_scales[:, cols],
                }
            )
        for g in range(H_PASSES):
            chunks.append(
                {
                    "table": "hid%d" % g,
                    "col_blk": out_blk,
                    "col_half": out_half,
                    "m": 0,
                    "rest": "hid%d_rest" % g,
                    "codes": w2_codes[:, g, :],
                    "scales": w2_scales[:, g, :],
                }
            )
        for c, chunk in enumerate(chunks):
            chunk["rows"] = w_rows[c]
            for name, dtype in (("clipped", BF16), ("log_n", F32), ("log_l", F32), ("diff", F32)):
                made = keep.tile([P, PACK, COLS], dtype, name="%s%d" % (name, c))
                chunk[name] = made
            grouped = keep.tile([P, COLS, PACK], BF16, name="grouped%d" % c, align_bytes=64)
            chunk["grouped"] = grouped

        def distances(c, u):
            chunk = chunks[c]
            m = chunk["m"] + u
            dist = dists.tile([P, 2, K_PASS], F32, name="dist")
            for xy in range(2):
                nc.vector.tensor_scalar(
                    out=dist[:, xy, :],
                    in0=pairs(chunk["table"])[:, :, xy],
                    scalar1=chunk["col_blk"][:, m, xy : xy + 1],
                    scalar2=chunk["col_half"][:, m, xy : xy + 1],
                    op0=ALU.max,
                    op1=ALU.subtract,
                )
            chunk["dist", u] = dist

        def turn(c, js):
            chunk = chunks[c]
            for j in js:
                length = ps_sum.tile([P, COLS], F32, name="length")
                chunk["length", j] = length
            for u in range(BLOCKS):
                for j in js:
                    k_cols = slice(j * P, (j + 1) * P)
                    terms = (
                        chunk["dist", u][:, 0, k_cols],
                        chunk["dist", u][:, 1, k_cols],
                        tables[chunk["rest"]][:, k_cols],
                    )
                    for i, term in enumerate(terms):
                        nc.tensor.matmul(
                            out=chunk["length", j][:, u * P : (u + 1) * P],
                            lhsT=term,
                            rhs=identity[:],
                            is_transpose=True,
                            start=(i == 0),
                            stop=(i == len(terms) - 1),
                        )

        def log_lengths(c, js):
            for j in js:
                nc.scalar.activation(
                    out=chunks[c]["log_l"][:, j, :],
                    in_=chunks[c]["length", j][:],
                    func=FUNC.Ln,
                    scale=L_SCALE,
                    bias=tiny[:],
                )

        def clip_weights(c):
            nc.vector.tensor_scalar(
                out=chunks[c]["clipped"][:],
                in0=chunks[c]["rows"][:],
                scalar1=-W_LIMIT,
                scalar2=W_LIMIT,
                op0=ALU.max,
                op1=ALU.min,
            )

        def log_widths(c):
            nc.scalar.activation(
                out=chunks[c]["log_n"][:],
                in_=chunks[c]["clipped"][:],
                func=FUNC.Ln,
                scale=N_SCALE,
                bias=n_bias[:],
            )

        def differences(c, js):
            rows = slice(js[0], js[-1] + 1)
            nc.vector.tensor_tensor(
                out=chunks[c]["diff"][:, rows, :],
                in0=chunks[c]["log_n"][:, rows, :],
                in1=chunks[c]["log_l"][:, rows, :],
                op=ALU.subtract,
            )

        def factors(c, half):
            cols = slice(half * HALF, (half + 1) * HALF)
            nc.scalar.activation(
                out=chunks[c]["log_l"][:, :, cols],
                in_=chunks[c]["diff"][:, :, cols],
                func=FUNC.Sigmoid,
            )

        def products(c, half):
            chunk = chunks[c]
            cols = slice(half * HALF, (half + 1) * HALF)
            nc.vector.tensor_tensor(
                out=chunk["grouped"][:, cols, :].rearrange("p (a i) j -> p a j i", i=4),
                in0=chunk["log_l"][:, :, cols].rearrange("p j (a i) -> p a j i", i=4),
                in1=chunk["rows"][:, :, cols].rearrange("p j (a i) -> p a j i", i=4),
                op=ALU.mult,
            )

        def quantise(c, half):
            cols = slice(half * HALF, (half + 1) * HALF)
            nc.vector.quantize_mx(
                out=chunks[c]["codes"][:, cols].bitcast(FP8X4),
                scales=chunks[c]["scales"][:, cols],
                in_=chunks[c]["grouped"][:, cols, :].rearrange("p c j -> p (c j)"),
            )

        x_grouped = keep.tile([P, B, PACK], BF16, align_bytes=64)
        hid_pre = keep.tile([P, H_PASSES, B, PACK], F32)
        hid_bf = keep.tile([P, H_PASSES, B * PACK], BF16, align_bytes=64)
        banks = {}

        def transpose_x():
            xT = psum.tile([P, PACK, B], BF16, name="xT", tag="hid0_then_x")
            for j in range(PACK):
                nc.tensor.transpose(
                    out=xT[:, j, :], in_=x_sb[:, j * P : (j + 1) * P], identity=identity_bf[:]
                )
            banks["xT"] = xT

        def group_x():
            nc.vector.tensor_copy(out=x_grouped[:], in_=banks["xT"][:].rearrange("p j b -> p b j"))

        def quantise_x():
            nc.vector.quantize_mx(
                out=x_codes[:].bitcast(FP8X4),
                scales=x_scales[:],
                in_=x_grouped[:].rearrange("p b j -> p (b j)"),
            )

        def first_product(g):
            hid_ps = psum.tile([P, PACK, B], F32, name="hid_ps%d" % g, tag="in_then_hid")
            for t in range(PACK):
                unit_cols = slice((g * PACK + t) * P, (g * PACK + t + 1) * P)
                nc.tensor.matmul_mx(
                    out=hid_ps[:, t, :],
                    lhsT=w1_codes[:, unit_cols].bitcast(FP8X4),
                    lhsT_scale=w1_scales[:, unit_cols],
                    rhs=x_codes[:].bitcast(FP8X4),
                    rhs_scale=x_scales[:],
                    start=True,
                    stop=True,
                )
            banks["hid", g] = hid_ps

        def add_b1(g):
            bias = b1_col[:, g * PACK : (g + 1) * PACK].unsqueeze(1).to_broadcast([P, B, PACK])
            nc.vector.tensor_tensor(
                out=hid_pre[:, g],
                in0=banks["hid", g][:].rearrange("q t b -> q b t"),
                in1=bias,
                op=ALU.add,
            )

        def hidden_sigmoid(g):
            nc.scalar.activation(
                out=hid_bf[:, g, :],
                in_=hid_pre[:, g].rearrange("q b t -> q (b t)"),
                func=FUNC.Sigmoid,
            )

        def quantise_hidden(g):
            nc.vector.quantize_mx(
                out=hid_codes[:, g, :].bitcast(FP8X4), scales=hid_scales[:, g, :], in_=hid_bf[:, g, :]
            )

        out_pre = keep.tile([P, O], F32)
        out_sb = keep.tile([P, O], F32)
        half_cols = [slice(half * HALF, (half + 1) * HALF) for half in range(2)]
        out_tags = ("hid1_then_out", "rest_then_out")

        def second_product(half):
            out_ps = psum.tile([P, HALF], F32, name="out_ps%d" % half, tag=out_tags[half])
            for g in range(H_PASSES):
                nc.tensor.matmul_mx(
                    out=out_ps[:],
                    lhsT=hid_codes[:, g, :].bitcast(FP8X4),
                    lhsT_scale=hid_scales[:, g, :],
                    rhs=w2_codes[:, g, half_cols[half]].bitcast(FP8X4),
                    rhs_scale=w2_scales[:, g, half_cols[half]],
                    start=(g == 0),
                    stop=(g == H_PASSES - 1),
                )
            banks["out", half] = out_ps

        def finish(half):
            o_cols = half_cols[half]
            nc.vector.tensor_tensor(
                out=out_pre[:, o_cols], in0=banks["out", half][:], in1=b2_row[:, o_cols], op=ALU.add
            )
            nc.scalar.activation(out=out_sb[:, o_cols], in_=out_pre[:, o_cols], func=FUNC.Sigmoid)
            nc.sync.dma_start(out=out[:, o_cols], in_=out_sb[:, o_cols])

        low, high = (0, 1), (2, 3)
        spread("in", "in_then_hid", words_of(in_blk), 0)
        keep_table("in")
        row_rests(in_rest, in_scaled, in_blk)
        spread("in_rest", "rest_then_out", in_rest, 0)
        times(hid_half[:], hid_blk[:], 0.5)
        distances(0, 0)
        distances(0, 1)
        keep_table("in_rest")
        clip_weights(0)
        log_widths(0)
        distances(0, 2)
        distances(0, 3)
        turn(0, low)
        turn(0, high)
        log_lengths(0, low)
        log_lengths(0, high)
        row_rests(hid_rest, hid_scaled, hid_blk)
        spread("hid0", "hid0_then_x", words_of(hid_blk), 0)
        spread("hid1", "hid1_then_out", words_of(hid_blk), PACK)
        spread("hid0_rest", "rest_then_out", hid_rest, 0)
        clip_weights(1)
        for u in range(BLOCKS):
            distances(1, u)
        turn(1, low)
        turn(1, high)
        keep_table("hid0")
        keep_table("hid0_rest")
        log_widths(1)
        times(out_half[:], out_blk[:], 0.5)
        differences(0, low)
        log_lengths(1, low)
        log_lengths(1, high)
        keep_table("hid1")
        spread("hid1_rest", "rest_then_out", hid_rest, PACK)
        keep_table("hid1_rest")
        clip_weights(2)
        log_widths(2)
        for u in range(BLOCKS):
            distances(2, u)
        turn(2, low)
        turn(2, high)
        differences(0, high)
        log_lengths(2, low)
        log_lengths(2, high)
        clip_weights(3)
        log_widths(3)
        for u in range(BLOCKS):
            distances(3, u)
        turn(3, low)
        turn(3, high)
        transpose_x()
        differences(1, low)
        differences(1, high)
        differences(2, low)
        differences(2, high)
        log_lengths(3, low)
        log_lengths(3, high)
        differences(3, low)
        group_x()
        differences(3, high)
        quantise_x()

        parts = [(c, half) for c in range(CHUNKS) for half in range(2)]
        for part in parts:
            factors(*part)
        products(*parts[0])
        products(*parts[1])
        quantise(*parts[0])
        products(*parts[2])
        quantise(*parts[1])
        first_product(0)
        products(*parts[3])
        quantise(*parts[2])
        products(*parts[4])
        quantise(*parts[3])
        first_product(1)
        add_b1(0)
        hidden_sigmoid(0)
        products(*parts[5])
        quantise(*parts[4])
        add_b1(1)
        hidden_sigmoid(1)
        products(*parts[6])
        quantise(*parts[5])
        quantise_hidden(0)
        products(*parts[7])
        quantise(*parts[6])
        quantise_hidden(1)
        second_product(0)
        quantise(*parts[7])
        second_product(1)
        finish(0)
        finish(1)
